import numpy as np
import ml_dtypes


def mxq(x, axis, fmt="e4m3"):
    dtype, down = {"e4m3": (ml_dtypes.float8_e4m3fn, 7), "e5m2": (ml_dtypes.float8_e5m2, 14)}[fmt]
    v = np.moveaxis(np.asarray(x, np.float32).astype(ml_dtypes.bfloat16).astype(np.float64), axis, -1)
    blocks = v.reshape(v.shape[:-1] + (-1, 32))
    amax = np.abs(blocks).max(-1, keepdims=True)
    byte = np.maximum(np.where(amax > 0, np.frexp(amax)[1] - 1 + 127, 0) - down, 1)
    scale = np.exp2(byte - 127.0)
    codes = (blocks / scale).astype(np.float32).astype(dtype).astype(np.float64)
    return np.moveaxis((codes * scale).reshape(v.shape), -1, axis)


WIDE = False


def mx_kscale(k):
    if not WIDE:
        return np.ones(k)
    levels = np.array([10, -10, 5, -5, 0])
    if k % 512:
        return np.exp2(np.random.permutation(np.resize(levels, k // 32))).repeat(32)
    a = np.empty((k // 512, 16))
    for p in range(k // 512):
        a[p, :8] = np.random.permutation(np.resize(levels, 8))
        for g in range(8):
            far = levels[np.abs(levels - a[p, g]) >= 10]
            a[p, g + 8] = far[np.random.randint(len(far))]
    return np.exp2(a.ravel()).repeat(32)


BF16 = ml_dtypes.bfloat16


def bf(x):
    return np.asarray(x, np.float32).astype(BF16)


def f64(x):
    return np.asarray(x).astype(np.float64)


S, B, H, NH, HD, ROT = 256, 1, 2048, 16, 128, 32
BASE = 10000.0
W3 = 3 * NH * HD


def rotate_half(x):
    x1, x2 = np.split(x, 2, axis=-1)
    return np.concatenate((-x2, x1), axis=-1)


def draw0():
    s = mx_kscale(H)
    return {"hidden_states": bf(np.random.standard_normal((S, B, H)) * s),
            "W_qkv": bf(np.random.standard_normal((W3, H)) / np.sqrt(H) / s[None, :]),
            "b_qkv": bf(np.random.standard_normal(W3) * 0.2)}


def core(hidden_states, W_qkv, b_qkv):
    x = f64(hidden_states)
    S_, B_ = x.shape[:2]
    qkv = (mxq(x, 2, "e4m3") @ mxq(f64(W_qkv), 1, "e4m3").T) + f64(b_qkv)
    qkv = qkv.reshape(S_, B_, NH, 3 * HD)
    q, k, v = qkv[..., :HD], qkv[..., HD:2 * HD], qkv[..., 2 * HD:]

    inv_freq = 1.0 / (BASE ** (np.arange(0, ROT, 2) / ROT))
    t = np.arange(S_)
    freqs = t[:, None] * inv_freq[None, :]
    emb = np.concatenate((freqs, freqs), axis=-1)
    cos = np.cos(emb)[:, None, None, :]
    sin = np.sin(emb)[:, None, None, :]

    def rope(u):
        return u * cos + rotate_half(u) * sin

    q = np.concatenate((rope(q[..., :ROT]), q[..., ROT:]), axis=-1)
    k = np.concatenate((rope(k[..., :ROT]), k[..., ROT:]), axis=-1)
    return q, k, v


def e4m3fn_bytes(y):
    return np.clip(np.asarray(y, np.float64), -448.0, 448.0).astype(np.float32).astype(ml_dtypes.float8_e4m3fn).view(np.uint8)


def e4m3fn_values(b):
    return np.asarray(b, np.uint8).view(ml_dtypes.float8_e4m3fn).astype(np.float64)


def setup_inputs():
    d = draw0()
    x0 = np.asarray(d['W_qkv']).astype(np.float64)
    s = (np.max(np.abs(x0), axis=(0,), keepdims=True) / 448.0).astype(np.float32)
    out = {}
    for k, v in d.items():
        if k == 'W_qkv':
            out['W_qkv_bytes'] = e4m3fn_bytes(x0 / s.astype(np.float64))
            out['W_qkv_scale'] = s
        else:
            out[k] = v
    return out


def reference(hidden_states, W_qkv_bytes, W_qkv_scale, b_qkv):
    return core(hidden_states, e4m3fn_values(W_qkv_bytes) * W_qkv_scale.astype(np.float64), b_qkv)

@@ -1,0 +1,279 @@
+from contextlib import ExitStack
+
+import concourse.mybir as mybir
+from concourse.masks import make_identity
+
+F32 = mybir.dt.float32
+BF16 = mybir.dt.bfloat16
+U32 = mybir.dt.uint32
+U8 = mybir.dt.uint8
+I32 = mybir.dt.int32
+FP8 = mybir.dt.float8_e4m3fn
+FP8X4 = mybir.dt.float8_e4m3fn_x4
+ACT = mybir.ActivationFunctionType
+ALU = mybir.AluOpType
+
+P = 128
+SEQ = 256
+HID = 2048
+NH = 16
+NT = 48
+PASSES = 4
+TWO_PI = 6.283185307179586
+
+FLOPS = 2 * SEQ * HID * 3 * NH * P
+
+PERM = True
+MANUAL = True
+
+
+def tile_selfattention_pa_kernel(tc, hidden_states, W_qkv_bytes, W_qkv_scale, b_qkv, out_0, out_1, out_2):
+    nc = tc.nc
+    outs = [out_0, out_1, out_2]
+    with ExitStack() as ctx:
+        const = ctx.enter_context(tc.tile_pool(name="const", bufs=1))
+        work = ctx.enter_context(tc.tile_pool(name="work", bufs=3))
+        ogp = ctx.enter_context(tc.tile_pool(name="ogp", bufs=2))
+        pst = ctx.enter_context(tc.psum_pool(name="pst", bufs=4))
+        psa = ctx.enter_context(tc.psum_pool(name="psa", bufs=2))
+        psb = ctx.enter_context(tc.psum_pool(name="psb", bufs=2))
+        if MANUAL:
+            ctx.enter_context(tc.manual_schedule())
+
+        wrows = W_qkv_bytes.rearrange("(i p) k -> p i k", p=P)
+        wv = {}
+
+        def load_w_single(h, c):
+            t = const.tile([P, HID], U8, name="wbytes_%d_%d" % (h, c))
+            nc.sync.dma_start(out=t[:], in_=wrows[:, 3 * h + c, :])
+            wv[(h, c)] = t[:]
+
+        def load_w_head(h):
+            t = const.tile([P, 3, HID], U8, name="wbytes_h%d" % h)
+            nc.sync.dma_start(out=t[:], in_=wrows[:, 3 * h:3 * h + 3, :])
+            for c in range(3):
+                wv[(h, c)] = t[:, c, :]
+
+        sc = const.tile([P, HID], F32, name="sc")
+        xraw = [const.tile([P, HID], BF16, name="xraw%d" % m) for m in range(2)]
+        xsrc = hidden_states.rearrange("(m p) b k -> p m (b k)", p=P)
+        braw = const.tile([P, P], BF16, name="braw")
+
+        pos_f = const.tile([P, 2], F32, name="pos_f")
+        nc.gpsimd.iota(pos_f[:], pattern=[[P, 2]], base=0, channel_multiplier=1, allow_small_or_imprecise_dtypes=True)
+        zero1 = const.tile([P, 1], F32, name="zero1")
+        nc.gpsimd.memset(zero1[:], 0.0)
+        nc.gpsimd.memset(braw[:], 0.0)
+        ident_f = const.tile([P, P], F32, name="ident_f")
+        make_identity(nc, ident_f[:])
+        ident_b = const.tile([P, P], BF16, name="ident_b")
+        make_identity(nc, ident_b[:])
+
+        load_w_single(0, 0)
+        nc.sync.dma_start(out=sc[:], in_=W_qkv_scale.rearrange("o k -> (o k)").partition_broadcast(P))
+        nc.sync.dma_start(out=braw[0:NT, :], in_=b_qkv.rearrange("(i d) -> i d", d=P))
+        load_w_single(0, 1)
+        for m in range(2):
+            nc.sync.dma_start(out=xraw[m][:], in_=xsrc[:, m, :])
+        load_w_head(1)
+        load_w_single(0, 2)
+        for h in range(2, NH):
+            load_w_head(h)
+
+        warm = const.tile([P, 1], F32, name="warm")
+        nc.scalar.activation(out=warm[:], in_=zero1[:], func=ACT.Sin)
+        turns = const.tile([P, 2, 16], F32, name="turns")
+        for j in range(16):
+            cj = (1.0 / (10000.0 ** (j / 16.0))) / TWO_PI
+            nc.scalar.activation(out=turns[:, :, j:j + 1], in_=pos_f[:].unsqueeze(2), func=ACT.Copy, scale=cj)
+        tflat = turns[:].rearrange("p m j -> p (m j)")
+        n_i = const.tile([P, 32], I32, name="n_i")
+        nc.vector.tensor_copy(out=n_i[:], in_=tflat)
+        n_f = const.tile([P, 32], F32, name="n_f")
+        nc.vector.tensor_copy(out=n_f[:], in_=n_i[:])
+        ang = const.tile([P, 2, 32], F32, name="ang")
+        nc.vector.tensor_tensor(out=ang[:, 0, :], in0=tflat, in1=n_f[:], op=ALU.subtract)
+        nc.vector.tensor_scalar(out=ang[:, 1, :], in0=ang[:, 0, :], scalar1=0.25, scalar2=None, op0=ALU.add)
+        aflat = ang[:].rearrange("p a j -> p (a j)")
+        wr1 = const.tile([P, 64], F32, name="wr1")
+        nc.vector.scalar_tensor_tensor(out=wr1[:], in0=aflat, scalar=0.5, in1=aflat, op0=ALU.is_gt, op1=ALU.subtract)
+        wr2 = const.tile([P, 2, 2, 16], F32, name="wr2")
+        nc.vector.scalar_tensor_tensor(out=wr2[:].rearrange("p a m j -> p (a m j)"), in0=wr1[:], scalar=0.5, in1=wr1[:],
+                                       op0=ALU.is_gt, op1=ALU.subtract)
+        cosT = const.tile([P, 2, 32], F32, name="cosT")
+        sinT = const.tile([P, 2, 32], F32, name="sinT")
+        nc.scalar.activation(out=cosT[:, :, 0:16], in_=wr2[:, 1, :, :], func=ACT.Sin, scale=TWO_PI)
+        nc.scalar.activation(out=cosT[:, :, 16:32], in_=wr2[:, 1, :, :], func=ACT.Sin, scale=TWO_PI)
+        nc.scalar.activation(out=sinT[:, :, 0:16], in_=wr2[:, 0, :, :], func=ACT.Sin, scale=-TWO_PI)
+        nc.scalar.activation(out=sinT[:, :, 16:32], in_=wr2[:, 0, :, :], func=ACT.Sin, scale=TWO_PI)
+
+        pbias = psb.tile([P, P], BF16, tag="pb")
+        nc.tensor.transpose(pbias[:], braw[:], ident_b[:])
+        bias = const.tile([P, NT], F32, name="bias")
+        nc.scalar.copy(out=bias[:], in_=pbias[:, 0:NT])
+
+        xg = const.tile([P, PASSES * SEQ * 4], BF16, name="xg", align_bytes=64)
+        xgw = xg[:].bitcast(F32).rearrange("p (g s u) -> p g s u", g=PASSES, u=2)
+        for m in range(2):
+            xw = xraw[m][:].bitcast(F32)
+            for hf in range(2):
+                pt = pst.tile([P, 2, 2, P], F32, tag="pt")
+                for gg in range(2):
+                    g = 2 * hf + gg
+                    for u in range(2):
+                        nc.tensor.transpose(pt[:, gg, u, :], xw[:, 256 * g + u:256 * (g + 1):2], ident_f[:])
+                nc.scalar.copy(out=xgw[:, 2 * hf:2 * hf + 2, m * P:(m + 1) * P, :], in_=pt[:].rearrange("p g u r -> p g r u"))
+        xcodes = const.tile([P, PASSES * SEQ], U32, name="xcodes", align_bytes=64)
+        xscl = const.tile([P, PASSES * SEQ], U8, name="xscl", align_bytes=64)
+
+        def quantize_x():
+            for hf in range(2):
+                nc.vector.quantize_mx(out=xcodes[:, 512 * hf:512 * (hf + 1)].bitcast(FP8X4),
+                                      scales=xscl[:, 512 * hf:512 * (hf + 1)],
+                                      in_=xg[:, 2048 * hf:2048 * (hf + 1)])
+
+        order = []
+        for hg in range(4):
+            for hh in range(4):
+                order.append((hg, hh, 0))
+                order.append((hg, hh, 1))
+            for hh in range(4):
+                order.append((hg, hh, 2))
+        wbf, wpm, grp, codes, scl, usb, og = {}, {}, {}, {}, {}, {}, {}
+        ptt, accs, pbs = {}, {}, {}
+        ov = [o.rearrange("(m p) b h d -> p m (b h) d", p=P) for o in outs]
+
+        def stage_tt(j):
+            hg, hh, c = order[j]
+            t = work.tile([P, HID], BF16, name="wbf", align_bytes=64)
+            nc.vector.tensor_tensor(out=t[:], in0=wv[(4 * hg + hh, c)].bitcast(FP8), in1=sc[:], op=ALU.mult)
+            wbf[j] = t
+
+        def stage_perm(j):
+            t = work.tile([P, HID], BF16, name="wpm", align_bytes=64)
+            nc.scalar.copy(out=t[:].bitcast(F32).rearrange("p (g u w) -> p g u w", g=PASSES, u=2),
+                           in_=wbf[j][:].bitcast(F32).rearrange("p (g w u) -> p g u w", g=PASSES, u=2))
+            wpm[j] = t
+
+        def stage_tr(j):
+            src = (wpm[j] if PERM else wbf[j])[:].bitcast(F32)
+            for hf in range(2):
+                pt = pst.tile([P, 2, 2, P], F32, tag="pt")
+                for gg in range(2):
+                    g = 2 * hf + gg
+                    for u in range(2):
+                        if PERM:
+                            in_ = src[:, (2 * g + u) * P:(2 * g + u + 1) * P]
+                        else:
+                            in_ = src[:, 256 * g + u:256 * (g + 1):2]
+                        nc.tensor.transpose(pt[:, gg, u, :], in_, ident_f[:])
+                ptt[(j, hf)] = pt
+
+        def stage_tr_exit(j):
+            t = work.tile([P, HID], BF16, name="grp", align_bytes=64)
+            tw = t[:].bitcast(F32).rearrange("p (g r u) -> p g r u", g=PASSES, u=2)
+            for hf in range(2):
+                nc.scalar.copy(out=tw[:, 2 * hf:2 * hf + 2, :, :], in_=ptt[(j, hf)][:].rearrange("p g u r -> p g r u"))
+            grp[j] = t
+
+        def stage_q(j):
+            cd = work.tile([P, PASSES * P], U32, name="codes", align_bytes=64)
+            sl = work.tile([P, PASSES * P], U8, name="scl", align_bytes=64)
+            nc.vector.quantize_mx(out=cd[:].bitcast(FP8X4), scales=sl[:], in_=grp[j][:])
+            codes[j] = cd
+            scl[j] = sl
+
+        def stage_mm(j):
+            hg, hh, c = order[j]
+            acc = psa.tile([P, SEQ], F32, tag="acc")
+            for g in range(PASSES):
+                nc.tensor.matmul_mx(out=acc[:],
+                                    lhsT=codes[j][:, g * P:(g + 1) * P].bitcast(FP8X4),
+                                    lhsT_scale=scl[j][:, g * P:(g + 1) * P],
+                                    rhs=xcodes[:, g * SEQ:(g + 1) * SEQ].bitcast(FP8X4),
+                                    rhs_scale=xscl[:, g * SEQ:(g + 1) * SEQ],
+                                    start=(g == 0), stop=(g == PASSES - 1))
+            accs[j] = acc
+
+        def stage_mm_exit(j):
+            hg, hh, c = order[j]
+            acc = accs[j]
+            u = work.tile([P, SEQ], F32, name="usb")
+            i = 3 * (4 * hg + hh) + c
+            nc.scalar.activation(out=u[:], in_=acc[:], func=ACT.Identity, bias=bias[:, i:i + 1], scale=1.0)
+            usb[j] = u
+
+        def stage_back_tr(j):
+            pb = psb.tile([P, 2, P], F32, tag="pb")
+            for m in range(2):
+                nc.tensor.transpose(pb[:, m, :], usb[j][:, m * P:(m + 1) * P], ident_f[:])
+            pbs[j] = pb
+
+        def stage_back_exit(j):
+            hg, hh, c = order[j]
+            if hg not in og:
+                og[hg] = ogp.tile([P, 2, 12, P], F32, name="og")
+            nc.scalar.copy(out=og[hg][:, :, 4 * c + hh, :], in_=pbs[j][:])
+
+        rtmp = {}
+
+        def rope_mul(hg):
+            o = og[hg]
+            ra = ogp.tile([P, 2, 8, 32], F32, name="ra")
+            rb = ogp.tile([P, 2, 8, 32], F32, name="rb")
+            nc.vector.tensor_tensor(out=rb[:, :, :, 0:16], in0=o[:, :, 0:8, 16:32],
+                                    in1=sinT[:, :, 0:16].unsqueeze(2).to_broadcast([P, 2, 8, 16]), op=ALU.mult)
+            nc.vector.tensor_tensor(out=rb[:, :, :, 16:32], in0=o[:, :, 0:8, 0:16],
+                                    in1=sinT[:, :, 16:32].unsqueeze(2).to_broadcast([P, 2, 8, 16]), op=ALU.mult)
+            nc.vector.tensor_tensor(out=ra[:], in0=o[:, :, 0:8, 0:32],
+                                    in1=cosT[:].unsqueeze(2).to_broadcast([P, 2, 8, 32]), op=ALU.mult)
+            rtmp[hg] = (ra, rb)
+
+        def rope_add_store(hg):
+            ra, rb = rtmp[hg]
+            nc.vector.tensor_tensor(out=og[hg][:, :, 0:8, 0:32], in0=ra[:], in1=rb[:], op=ALU.add)
+            for c in range(2):
+                nc.sync.dma_start(out=ov[c][:, :, 4 * hg:4 * hg + 4, :], in_=og[hg][:, :, 4 * c:4 * c + 4, :])
+
+        def store_v(hg):
+            nc.sync.dma_start(out=ov[2][:, :, 4 * hg:4 * hg + 4, :], in_=og[hg][:, :, 8:12, :])
+
+        d_perm = 1
+        d_tr = 2 if PERM else 1
+        d_ex = d_tr + 1
+        d_q = d_ex + 1
+        d_mm = d_q + 1
+        d_e1 = d_mm + 1
+        d_bt = d_e1 + 1
+        d_back = d_bt + 1
+        for it in range(NT + d_back + 2):
+            if it < NT:
+                stage_tt(it)
+            if it == d_q:
+                quantize_x()
+            if 0 <= it - d_back < NT:
+                stage_back_exit(it - d_back)
+            if 0 <= it - d_bt < NT:
+                stage_back_tr(it - d_bt)
+            if PERM and 0 <= it - d_perm < NT:
+                stage_perm(it - d_perm)
+            if 0 <= it - d_ex < NT:
+                stage_tr_exit(it - d_ex)
+            if 0 <= it - d_tr < NT:
+                stage_tr(it - d_tr)
+            if 0 <= it - d_e1 < NT:
+                stage_mm_exit(it - d_e1)
+            if 0 <= it - d_mm < NT:
+                stage_mm(it - d_mm)
+            if 0 <= it - d_q < NT:
+                stage_q(it - d_q)
+            jb = it - d_back
+            if jb >= 0 and jb % 12 == 7:
+                rope_mul(jb // 12)
+            if jb >= 0 and jb % 12 == 8:
+                rope_add_store(jb // 12)
+            if 0 <= jb < 36 and jb % 12 == 11:
+                store_v(jb // 12)
+            if 44 <= jb < NT:
+                hl = jb - 44
+                nc.sync.dma_start(out=ov[2][:, :, 12 + hl, :], in_=og[3][:, :, 8 + hl, :])

@@ -23,8 +23,10 @@ TWO_PI = 6.283185307179586
 
 FLOPS = 2 * SEQ * HID * 3 * NH * P
 
-PERM = True
 MANUAL = True
+HEAD_CHUNKS = False
+NPERM = 3
+TAIL_ORDER = False
 
 
 def tile_selfattention_pa_kernel(tc, hidden_states, W_qkv_bytes, W_qkv_scale, b_qkv, out_0, out_1, out_2):
@@ -70,7 +72,12 @@ def tile_selfattention_pa_kernel(tc, hidden_states, W_qkv_bytes, W_qkv_scale, b_
         make_identity(nc, ident_b[:])
 
         load_w_single(0, 0)
-        nc.sync.dma_start(out=sc[:], in_=W_qkv_scale.rearrange("o k -> (o k)").partition_broadcast(P))
+        sflat = W_qkv_scale.rearrange("o k -> (o k)")
+        if HEAD_CHUNKS:
+            for q4 in range(4):
+                nc.sync.dma_start(out=sc[:, 512 * q4:512 * (q4 + 1)], in_=sflat[512 * q4:512 * (q4 + 1)].partition_broadcast(P))
+        else:
+            nc.sync.dma_start(out=sc[:], in_=sflat.partition_broadcast(P))
         nc.sync.dma_start(out=braw[0:NT, :], in_=b_qkv.rearrange("(i d) -> i d", d=P))
         load_w_single(0, 1)
         for m in range(2):
@@ -133,12 +140,20 @@ def tile_selfattention_pa_kernel(tc, hidden_states, W_qkv_bytes, W_qkv_scale, b_
                                       in_=xg[:, 2048 * hf:2048 * (hf + 1)])
 
         order = []
-        for hg in range(4):
+        blocks = [(0, 0), (0, 2), (1, 0), (1, 2), (2, 0), (3, 0), (2, 2), (3, 2)] if TAIL_ORDER else [
+            (0, 0), (0, 2), (1, 0), (1, 2), (2, 0), (2, 2), (3, 0), (3, 2)]
+        qk_done, v_done = {}, {}
+        for hg, kind in blocks:
             for hh in range(4):
-                order.append((hg, hh, 0))
-                order.append((hg, hh, 1))
-            for hh in range(4):
-                order.append((hg, hh, 2))
+                if kind == 0:
+                    order.append((hg, hh, 0))
+                    order.append((hg, hh, 1))
+                else:
+                    order.append((hg, hh, 2))
+            if kind == 0:
+                qk_done[len(order) - 1] = hg
+            else:
+                v_done[len(order) - 1] = hg
         wbf, wpm, grp, codes, scl, usb, og = {}, {}, {}, {}, {}, {}, {}
         ptt, accs, pbs = {}, {}, {}
         ov = [o.rearrange("(m p) b h d -> p m (b h) d", p=P) for o in outs]
@@ -146,26 +161,35 @@ def tile_selfattention_pa_kernel(tc, hidden_states, W_qkv_bytes, W_qkv_scale, b_
         def stage_tt(j):
             hg, hh, c = order[j]
             t = work.tile([P, HID], BF16, name="wbf", align_bytes=64)
-            nc.vector.tensor_tensor(out=t[:], in0=wv[(4 * hg + hh, c)].bitcast(FP8), in1=sc[:], op=ALU.mult)
+            nparts = 4 if (HEAD_CHUNKS and j == 0) else 1
+            wd = HID // nparts
+            for q4 in range(nparts):
+                cs = slice(wd * q4, wd * (q4 + 1))
+                nc.vector.tensor_tensor(out=t[:, cs], in0=wv[(4 * hg + hh, c)][:, cs].bitcast(FP8), in1=sc[:, cs], op=ALU.mult)
             wbf[j] = t
 
         def stage_perm(j):
             t = work.tile([P, HID], BF16, name="wpm", align_bytes=64)
-            nc.scalar.copy(out=t[:].bitcast(F32).rearrange("p (g u w) -> p g u w", g=PASSES, u=2),
-                           in_=wbf[j][:].bitcast(F32).rearrange("p (g w u) -> p g u w", g=PASSES, u=2))
+            tw = t[:].bitcast(F32)
+            sw = wbf[j][:].bitcast(F32)
+            ranges = [(g, g + 1) for g in range(NPERM)] if (HEAD_CHUNKS and j == 0) else [(0, NPERM)]
+            for g0, g1 in ranges:
+                nc.scalar.copy(out=tw[:, 256 * g0:256 * g1].rearrange("p (g u w) -> p g u w", g=g1 - g0, u=2),
+                               in_=sw[:, 256 * g0:256 * g1].rearrange("p (g w u) -> p g u w", g=g1 - g0, u=2))
             wpm[j] = t
 
         def stage_tr(j):
-            src = (wpm[j] if PERM else wbf[j])[:].bitcast(F32)
+            src = wpm[j][:].bitcast(F32)
+            raw = wbf[j][:].bitcast(F32)
             for hf in range(2):
                 pt = pst.tile([P, 2, 2, P], F32, tag="pt")
                 for gg in range(2):
                     g = 2 * hf + gg
                     for u in range(2):
-                        if PERM:
+                        if g < NPERM:
                             in_ = src[:, (2 * g + u) * P:(2 * g + u + 1) * P]
                         else:
-                            in_ = src[:, 256 * g + u:256 * (g + 1):2]
+                            in_ = raw[:, 256 * g + u:256 * (g + 1):2]
                         nc.tensor.transpose(pt[:, gg, u, :], in_, ident_f[:])
                 ptt[(j, hf)] = pt
 
@@ -239,7 +263,7 @@ def tile_selfattention_pa_kernel(tc, hidden_states, W_qkv_bytes, W_qkv_scale, b_
             nc.sync.dma_start(out=ov[2][:, :, 4 * hg:4 * hg + 4, :], in_=og[hg][:, :, 8:12, :])
 
         d_perm = 1
-        d_tr = 2 if PERM else 1
+        d_tr = 2
         d_ex = d_tr + 1
         d_q = d_ex + 1
         d_mm = d_q + 1
@@ -255,7 +279,7 @@ def tile_selfattention_pa_kernel(tc, hidden_states, W_qkv_bytes, W_qkv_scale, b_
                 stage_back_exit(it - d_back)
             if 0 <= it - d_bt < NT:
                 stage_back_tr(it - d_bt)
-            if PERM and 0 <= it - d_perm < NT:
+            if 0 <= it - d_perm < NT:
                 stage_perm(it - d_perm)
             if 0 <= it - d_ex < NT:
                 stage_tr_exit(it - d_ex)
@@ -268,12 +292,12 @@ def tile_selfattention_pa_kernel(tc, hidden_states, W_qkv_bytes, W_qkv_scale, b_
             if 0 <= it - d_q < NT:
                 stage_q(it - d_q)
             jb = it - d_back
-            if jb >= 0 and jb % 12 == 7:
-                rope_mul(jb // 12)
-            if jb >= 0 and jb % 12 == 8:
-                rope_add_store(jb // 12)
-            if 0 <= jb < 36 and jb % 12 == 11:
-                store_v(jb // 12)
+            if jb in qk_done:
+                rope_mul(qk_done[jb])
+            if jb - 1 in qk_done:
+                rope_add_store(qk_done[jb - 1])
+            if jb in v_done and v_done[jb] != 3:
+                store_v(v_done[jb])
             if 44 <= jb < NT:
                 hl = jb - 44
                 nc.sync.dma_start(out=ov[2][:, :, 12 + hl, :], in_=og[3][:, :, 8 + hl, :])

@@ -25,7 +25,7 @@ FLOPS = 2 * SEQ * HID * 3 * NH * P
 
 MANUAL = True
 HEAD_CHUNKS = False
-NPERM = 3
+NPERM = 2
 TAIL_ORDER = False
 
 

@@ -25,7 +25,8 @@ FLOPS = 2 * SEQ * HID * 3 * NH * P
 
 MANUAL = True
 HEAD_CHUNKS = False
-NPERM = 2
+NPERM = 0
+BACK_MM = True
 TAIL_ORDER = False
 
 
@@ -178,10 +179,10 @@ def tile_selfattention_pa_kernel(tc, hidden_states, W_qkv_bytes, W_qkv_scale, b_
                                in_=sw[:, 256 * g0:256 * g1].rearrange("p (g w u) -> p g u w", g=g1 - g0, u=2))
             wpm[j] = t
 
-        def stage_tr(j):
-            src = wpm[j][:].bitcast(F32)
+        def stage_tr(j, hfs):
+            src = wpm[j][:].bitcast(F32) if NPERM > 0 else None
             raw = wbf[j][:].bitcast(F32)
-            for hf in range(2):
+            for hf in hfs:
                 pt = pst.tile([P, 2, 2, P], F32, tag="pt")
                 for gg in range(2):
                     g = 2 * hf + gg
@@ -230,7 +231,10 @@ def tile_selfattention_pa_kernel(tc, hidden_states, W_qkv_bytes, W_qkv_scale, b_
         def stage_back_tr(j):
             pb = psb.tile([P, 2, P], F32, tag="pb")
             for m in range(2):
-                nc.tensor.transpose(pb[:, m, :], usb[j][:, m * P:(m + 1) * P], ident_f[:])
+                if BACK_MM:
+                    nc.tensor.matmul(pb[:, m, :], lhsT=usb[j][:, m * P:(m + 1) * P], rhs=ident_f[:], start=True, stop=True)
+                else:
+                    nc.tensor.transpose(pb[:, m, :], usb[j][:, m * P:(m + 1) * P], ident_f[:])
             pbs[j] = pb
 
         def stage_back_exit(j):
@@ -277,18 +281,20 @@ def tile_selfattention_pa_kernel(tc, hidden_states, W_qkv_bytes, W_qkv_scale, b_
                 quantize_x()
             if 0 <= it - d_back < NT:
                 stage_back_exit(it - d_back)
-            if 0 <= it - d_bt < NT:
-                stage_back_tr(it - d_bt)
-            if 0 <= it - d_perm < NT:
+            if NPERM > 0 and 0 <= it - d_perm < NT:
                 stage_perm(it - d_perm)
             if 0 <= it - d_ex < NT:
                 stage_tr_exit(it - d_ex)
             if 0 <= it - d_tr < NT:
-                stage_tr(it - d_tr)
+                stage_tr(it - d_tr, [0])
             if 0 <= it - d_e1 < NT:
                 stage_mm_exit(it - d_e1)
             if 0 <= it - d_mm < NT:
                 stage_mm(it - d_mm)
+            if 0 <= it - d_tr < NT:
+                stage_tr(it - d_tr, [1])
+            if 0 <= it - d_bt < NT:
+                stage_back_tr(it - d_bt)
             if 0 <= it - d_q < NT:
                 stage_q(it - d_q)
             jb = it - d_back

@@ -23,11 +23,8 @@ TWO_PI = 6.283185307179586
 
 FLOPS = 2 * SEQ * HID * 3 * NH * P
 
-MANUAL = True
-HEAD_CHUNKS = False
-NPERM = 0
-BACK_MM = True
-TAIL_ORDER = False
+PB_POS = (8, 20, 30, 40)
+DELTA = 4
 
 
 def tile_selfattention_pa_kernel(tc, hidden_states, W_qkv_bytes, W_qkv_scale, b_qkv, out_0, out_1, out_2):
@@ -36,12 +33,13 @@ def tile_selfattention_pa_kernel(tc, hidden_states, W_qkv_bytes, W_qkv_scale, b_
     with ExitStack() as ctx:
         const = ctx.enter_context(tc.tile_pool(name="const", bufs=1))
         work = ctx.enter_context(tc.tile_pool(name="work", bufs=3))
+        deep = ctx.enter_context(tc.tile_pool(name="deep", bufs=4))
+        pbp = ctx.enter_context(tc.tile_pool(name="pbp", bufs=1))
         ogp = ctx.enter_context(tc.tile_pool(name="ogp", bufs=2))
         pst = ctx.enter_context(tc.psum_pool(name="pst", bufs=4))
         psa = ctx.enter_context(tc.psum_pool(name="psa", bufs=2))
         psb = ctx.enter_context(tc.psum_pool(name="psb", bufs=2))
-        if MANUAL:
-            ctx.enter_context(tc.manual_schedule())
+        ctx.enter_context(tc.manual_schedule())
 
         wrows = W_qkv_bytes.rearrange("(i p) k -> p i k", p=P)
         wv = {}
@@ -74,13 +72,11 @@ def tile_selfattention_pa_kernel(tc, hidden_states, W_qkv_bytes, W_qkv_scale, b_
 
         load_w_single(0, 0)
         sflat = W_qkv_scale.rearrange("o k -> (o k)")
-        if HEAD_CHUNKS:
-            for q4 in range(4):
-                nc.sync.dma_start(out=sc[:, 512 * q4:512 * (q4 + 1)], in_=sflat[512 * q4:512 * (q4 + 1)].partition_broadcast(P))
-        else:
-            nc.sync.dma_start(out=sc[:], in_=sflat.partition_broadcast(P))
+        nc.sync.dma_start(out=sc[:], in_=sflat.partition_broadcast(P))
         nc.sync.dma_start(out=braw[0:NT, :], in_=b_qkv.rearrange("(i d) -> i d", d=P))
         load_w_single(0, 1)
+        scol = const.tile([P, 4 * PASSES], F32, name="scol")
+        nc.sync.dma_start(out=scol[:].rearrange("p (g t) -> p g t", t=4), in_=W_qkv_scale.rearrange("o (g p t) -> p (o g) t", p=P, t=4))
         for m in range(2):
             nc.sync.dma_start(out=xraw[m][:], in_=xsrc[:, m, :])
         load_w_head(1)
@@ -141,65 +137,76 @@ def tile_selfattention_pa_kernel(tc, hidden_states, W_qkv_bytes, W_qkv_scale, b_
                                       in_=xg[:, 2048 * hf:2048 * (hf + 1)])
 
         order = []
-        blocks = [(0, 0), (0, 2), (1, 0), (1, 2), (2, 0), (3, 0), (2, 2), (3, 2)] if TAIL_ORDER else [
-            (0, 0), (0, 2), (1, 0), (1, 2), (2, 0), (2, 2), (3, 0), (3, 2)]
-        qk_done, v_done = {}, {}
-        for hg, kind in blocks:
+        for hg, kind in [(0, 0), (0, 2), (1, 0), (1, 2), (2, 0), (3, 0), (2, 2), (3, 2)]:
             for hh in range(4):
                 if kind == 0:
                     order.append((hg, hh, 0))
                     order.append((hg, hh, 1))
                 else:
                     order.append((hg, hh, 2))
-            if kind == 0:
-                qk_done[len(order) - 1] = hg
-            else:
-                v_done[len(order) - 1] = hg
-        wbf, wpm, grp, codes, scl, usb, og = {}, {}, {}, {}, {}, {}, {}
+        down = []
+        for idx in range(NT):
+            if idx not in PB_POS:
+                down.append(idx)
+            if idx - DELTA in PB_POS:
+                down.append(idx - DELTA)
+        assert len(down) == NT
+        wbf, cbs, pls, grp, codes, scl, usb, og = {}, {}, {}, {}, {}, {}, {}, {}
         ptt, accs, pbs = {}, {}, {}
         ov = [o.rearrange("(m p) b h d -> p m (b h) d", p=P) for o in outs]
 
-        def stage_tt(j):
+        def wbytes(j):
             hg, hh, c = order[j]
-            t = work.tile([P, HID], BF16, name="wbf", align_bytes=64)
-            nparts = 4 if (HEAD_CHUNKS and j == 0) else 1
-            wd = HID // nparts
-            for q4 in range(nparts):
-                cs = slice(wd * q4, wd * (q4 + 1))
-                nc.vector.tensor_tensor(out=t[:, cs], in0=wv[(4 * hg + hh, c)][:, cs].bitcast(FP8), in1=sc[:, cs], op=ALU.mult)
+            return wv[(4 * hg + hh, c)]
+
+        def stage_tt(j):
+            t = deep.tile([P, HID], BF16, name="wbf", align_bytes=64)
+            nc.vector.tensor_tensor(out=t[:], in0=wbytes(j).bitcast(FP8), in1=sc[:], op=ALU.mult)
             wbf[j] = t
 
-        def stage_perm(j):
-            t = work.tile([P, HID], BF16, name="wpm", align_bytes=64)
-            tw = t[:].bitcast(F32)
-            sw = wbf[j][:].bitcast(F32)
-            ranges = [(g, g + 1) for g in range(NPERM)] if (HEAD_CHUNKS and j == 0) else [(0, NPERM)]
-            for g0, g1 in ranges:
-                nc.scalar.copy(out=tw[:, 256 * g0:256 * g1].rearrange("p (g u w) -> p g u w", g=g1 - g0, u=2),
-                               in_=sw[:, 256 * g0:256 * g1].rearrange("p (g w u) -> p g u w", g=g1 - g0, u=2))
-            wpm[j] = t
+        def stage_cast(j, q4):
+            if q4 == 0:
+                cbs[j] = pbp.tile([P, HID], BF16, name="cb")
+            cs = slice(512 * q4, 512 * (q4 + 1))
+            nc.scalar.copy(out=cbs[j][:, cs], in_=wbytes(j)[:, cs].bitcast(FP8))
 
-        def stage_tr(j, hfs):
-            src = wpm[j][:].bitcast(F32) if NPERM > 0 else None
-            raw = wbf[j][:].bitcast(F32)
-            for hf in hfs:
+        def stage_tr(j, hf):
+            if j in PB_POS:
+                pt = pst.tile([P, 2, 4, P], BF16, tag="pt")
+                for gg in range(2):
+                    g = 2 * hf + gg
+                    for t in range(4):
+                        nc.tensor.transpose(pt[:, gg, t, :], cbs[j][:, 512 * g + t:512 * (g + 1):4], ident_b[:])
+            else:
+                raw = wbf[j][:].bitcast(F32)
                 pt = pst.tile([P, 2, 2, P], F32, tag="pt")
                 for gg in range(2):
                     g = 2 * hf + gg
                     for u in range(2):
-                        if g < NPERM:
-                            in_ = src[:, (2 * g + u) * P:(2 * g + u + 1) * P]
-                        else:
-                            in_ = raw[:, 256 * g + u:256 * (g + 1):2]
-                        nc.tensor.transpose(pt[:, gg, u, :], in_, ident_f[:])
-                ptt[(j, hf)] = pt
+                        nc.tensor.transpose(pt[:, gg, u, :], raw[:, 256 * g + u:256 * (g + 1):2], ident_f[:])
+            ptt[(j, hf)] = pt
 
         def stage_tr_exit(j):
-            t = work.tile([P, HID], BF16, name="grp", align_bytes=64)
+            t = deep.tile([P, HID], BF16, name="grp", align_bytes=64)
             tw = t[:].bitcast(F32).rearrange("p (g r u) -> p g r u", g=PASSES, u=2)
             for hf in range(2):
                 nc.scalar.copy(out=tw[:, 2 * hf:2 * hf + 2, :, :], in_=ptt[(j, hf)][:].rearrange("p g u r -> p g r u"))
             grp[j] = t
+
+        def stage_pb_exit(j, hf):
+            if hf == 0:
+                pls[j] = pbp.tile([P, PASSES, 4, P], BF16, name="pl")
+            for gg in range(2):
+                g = 2 * hf + gg
+                for t in range(4):
+                    nc.scalar.activation(out=pls[j][:, g, t, :], in_=ptt[(j, hf)][:, gg, t, :], func=ACT.Copy,
+                                         scale=scol[:, 4 * g + t:4 * g + t + 1])
+
+        def stage_pb_weave(j, g):
+            if g == 0:
+                grp[j] = pbp.tile([P, HID], BF16, name="grpb", align_bytes=64)
+            nc.scalar.copy(out=grp[j][:, 512 * g:512 * (g + 1)].rearrange("p (r t) -> p r t", t=4),
+                           in_=pls[j][:, g, :, :].rearrange("p t r -> p r t"))
 
         def stage_q(j):
             cd = work.tile([P, PASSES * P], U32, name="codes", align_bytes=64)
@@ -209,7 +216,6 @@ def tile_selfattention_pa_kernel(tc, hidden_states, W_qkv_bytes, W_qkv_scale, b_
             scl[j] = sl
 
         def stage_mm(j):
-            hg, hh, c = order[j]
             acc = psa.tile([P, SEQ], F32, tag="acc")
             for g in range(PASSES):
                 nc.tensor.matmul_mx(out=acc[:],
@@ -222,88 +228,107 @@ def tile_selfattention_pa_kernel(tc, hidden_states, W_qkv_bytes, W_qkv_scale, b_
 
         def stage_mm_exit(j):
             hg, hh, c = order[j]
-            acc = accs[j]
             u = work.tile([P, SEQ], F32, name="usb")
             i = 3 * (4 * hg + hh) + c
-            nc.scalar.activation(out=u[:], in_=acc[:], func=ACT.Identity, bias=bias[:, i:i + 1], scale=1.0)
+            nc.scalar.activation(out=u[:], in_=accs[j][:], func=ACT.Identity, bias=bias[:, i:i + 1], scale=1.0)
             usb[j] = u
 
-        def stage_back_tr(j):
+        def stage_back(j):
             pb = psb.tile([P, 2, P], F32, tag="pb")
             for m in range(2):
-                if BACK_MM:
-                    nc.tensor.matmul(pb[:, m, :], lhsT=usb[j][:, m * P:(m + 1) * P], rhs=ident_f[:], start=True, stop=True)
-                else:
-                    nc.tensor.transpose(pb[:, m, :], usb[j][:, m * P:(m + 1) * P], ident_f[:])
+                nc.tensor.matmul(pb[:, m, :], lhsT=usb[j][:, m * P:(m + 1) * P], rhs=ident_f[:], start=True, stop=True)
             pbs[j] = pb
+
+        v_count = {}
 
         def stage_back_exit(j):
             hg, hh, c = order[j]
             if hg not in og:
                 og[hg] = ogp.tile([P, 2, 12, P], F32, name="og")
             nc.scalar.copy(out=og[hg][:, :, 4 * c + hh, :], in_=pbs[j][:])
+            if c == 2:
+                if hg == 3:
+                    nc.sync.dma_start(out=ov[2][:, :, 12 + hh, :], in_=og[3][:, :, 8 + hh, :])
+                else:
+                    v_count[hg] = v_count.get(hg, 0) + 1
+                    if v_count[hg] == 4:
+                        nc.sync.dma_start(out=ov[2][:, :, 4 * hg:4 * hg + 4, :], in_=og[hg][:, :, 8:12, :])
 
         rtmp = {}
 
-        def rope_mul(hg):
+        def rope_mul(hg, c0, c1):
             o = og[hg]
-            ra = ogp.tile([P, 2, 8, 32], F32, name="ra")
-            rb = ogp.tile([P, 2, 8, 32], F32, name="rb")
-            nc.vector.tensor_tensor(out=rb[:, :, :, 0:16], in0=o[:, :, 0:8, 16:32],
-                                    in1=sinT[:, :, 0:16].unsqueeze(2).to_broadcast([P, 2, 8, 16]), op=ALU.mult)
-            nc.vector.tensor_tensor(out=rb[:, :, :, 16:32], in0=o[:, :, 0:8, 0:16],
-                                    in1=sinT[:, :, 16:32].unsqueeze(2).to_broadcast([P, 2, 8, 16]), op=ALU.mult)
-            nc.vector.tensor_tensor(out=ra[:], in0=o[:, :, 0:8, 0:32],
-                                    in1=cosT[:].unsqueeze(2).to_broadcast([P, 2, 8, 32]), op=ALU.mult)
-            rtmp[hg] = (ra, rb)
+            n = 4 * (c1 - c0)
+            ts = slice(4 * c0, 4 * c1)
+            ra = ogp.tile([P, 2, n, 32], F32, name="ra")
+            rb = ogp.tile([P, 2, n, 32], F32, name="rb")
+            nc.vector.tensor_tensor(out=rb[:, :, :, 0:16], in0=o[:, :, ts, 16:32],
+                                    in1=sinT[:, :, 0:16].unsqueeze(2).to_broadcast([P, 2, n, 16]), op=ALU.mult)
+            nc.vector.tensor_tensor(out=rb[:, :, :, 16:32], in0=o[:, :, ts, 0:16],
+                                    in1=sinT[:, :, 16:32].unsqueeze(2).to_broadcast([P, 2, n, 16]), op=ALU.mult)
+            nc.vector.tensor_tensor(out=ra[:], in0=o[:, :, ts, 0:32],
+                                    in1=cosT[:].unsqueeze(2).to_broadcast([P, 2, n, 32]), op=ALU.mult)
+            rtmp[(hg, c0)] = (ra, rb)
 
-        def rope_add_store(hg):
-            ra, rb = rtmp[hg]
-            nc.vector.tensor_tensor(out=og[hg][:, :, 0:8, 0:32], in0=ra[:], in1=rb[:], op=ALU.add)
-            for c in range(2):
+        def rope_add_store(hg, c0, c1):
+            ra, rb = rtmp[(hg, c0)]
+            nc.vector.tensor_tensor(out=og[hg][:, :, 4 * c0:4 * c1, 0:32], in0=ra[:], in1=rb[:], op=ALU.add)
+            for c in range(c0, c1):
                 nc.sync.dma_start(out=ov[c][:, :, 4 * hg:4 * hg + 4, :], in_=og[hg][:, :, 4 * c:4 * c + 4, :])
 
-        def store_v(hg):
-            nc.sync.dma_start(out=ov[2][:, :, 4 * hg:4 * hg + 4, :], in_=og[hg][:, :, 8:12, :])
-
-        d_perm = 1
-        d_tr = 2
-        d_ex = d_tr + 1
-        d_q = d_ex + 1
-        d_mm = d_q + 1
-        d_e1 = d_mm + 1
-        d_bt = d_e1 + 1
-        d_back = d_bt + 1
-        for it in range(NT + d_back + 2):
-            if it < NT:
+        d_tr = 1
+        d_ex = 2
+        d_q = 4
+        d_mm = 5
+        d_e1 = 6
+        d_bt = 7
+        d_back = 8
+        rope_at = {}
+        qk_count = {}
+        for di in range(NT):
+            hg, hh, c = order[down[di]]
+            if c < 2:
+                qk_count[hg] = qk_count.get(hg, 0) + 1
+                if qk_count[hg] == 8 and hg < 2:
+                    rope_at[di + d_back] = [(0, hg, 0, 2)]
+                    rope_at[di + d_back + 1] = [(1, hg, 0, 2)]
+        rope_at[NT] = [(0, 2, 0, 1)]
+        rope_at[NT + 1] = [(1, 2, 0, 1), (0, 2, 1, 2)]
+        rope_at[NT + 2] = [(1, 2, 1, 2)]
+        rope_at[NT + 3] = [(0, 3, 0, 1), (0, 3, 1, 2), (1, 3, 0, 1), (1, 3, 1, 2)]
+        for it in range(NT + d_back + 1):
+            if it < NT and it not in PB_POS:
                 stage_tt(it)
             if it == d_q:
                 quantize_x()
-            if 0 <= it - d_back < NT:
-                stage_back_exit(it - d_back)
-            if NPERM > 0 and 0 <= it - d_perm < NT:
-                stage_perm(it - d_perm)
-            if 0 <= it - d_ex < NT:
-                stage_tr_exit(it - d_ex)
-            if 0 <= it - d_tr < NT:
-                stage_tr(it - d_tr, [0])
             if 0 <= it - d_e1 < NT:
-                stage_mm_exit(it - d_e1)
-            if 0 <= it - d_mm < NT:
-                stage_mm(it - d_mm)
+                stage_mm_exit(down[it - d_e1])
+            if 0 <= it - d_back < NT:
+                stage_back_exit(down[it - d_back])
+            if it - d_ex - 1 in PB_POS:
+                stage_pb_exit(it - d_ex - 1, 1)
+            if 0 <= it - d_ex < NT:
+                if it - d_ex in PB_POS:
+                    stage_pb_exit(it - d_ex, 0)
+                else:
+                    stage_tr_exit(it - d_ex)
+            for j0 in PB_POS:
+                if 1 <= j0 - it <= 4:
+                    stage_cast(j0, 4 - (j0 - it))
+                if 4 <= it - j0 <= 7:
+                    stage_pb_weave(j0, it - j0 - 4)
             if 0 <= it - d_tr < NT:
-                stage_tr(it - d_tr, [1])
+                stage_tr(it - d_tr, 0)
+            if 0 <= it - d_mm < NT:
+                stage_mm(down[it - d_mm])
+            if 0 <= it - d_tr < NT:
+                stage_tr(it - d_tr, 1)
             if 0 <= it - d_bt < NT:
-                stage_back_tr(it - d_bt)
+                stage_back(down[it - d_bt])
             if 0 <= it - d_q < NT:
-                stage_q(it - d_q)
-            jb = it - d_back
-            if jb in qk_done:
-                rope_mul(qk_done[jb])
-            if jb - 1 in qk_done:
-                rope_add_store(qk_done[jb - 1])
-            if jb in v_done and v_done[jb] != 3:
-                store_v(v_done[jb])
-            if 44 <= jb < NT:
-                hl = jb - 44
-                nc.sync.dma_start(out=ov[2][:, :, 12 + hl, :], in_=og[3][:, :, 8 + hl, :])
+                stage_q(down[it - d_q])
+            for act, hg, c0, c1 in rope_at.get(it, []):
+                if act == 0:
+                    rope_mul(hg, c0, c1)
+                else:
+                    rope_add_store(hg, c0, c1)

@@ -23,7 +23,7 @@ TWO_PI = 6.283185307179586
 
 FLOPS = 2 * SEQ * HID * 3 * NH * P
 
-PB_POS = (8, 20, 30, 40)
+PB_POS = (0, 10, 20, 30, 40)
 DELTA = 4
 
 
@@ -70,11 +70,11 @@ def tile_selfattention_pa_kernel(tc, hidden_states, W_qkv_bytes, W_qkv_scale, b_
         ident_b = const.tile([P, P], BF16, name="ident_b")
         make_identity(nc, ident_b[:])
 
-        load_w_single(0, 0)
+        load_w_single(0, 1)
         sflat = W_qkv_scale.rearrange("o k -> (o k)")
         nc.sync.dma_start(out=sc[:], in_=sflat.partition_broadcast(P))
         nc.sync.dma_start(out=braw[0:NT, :], in_=b_qkv.rearrange("(i d) -> i d", d=P))
-        load_w_single(0, 1)
+        load_w_single(0, 0)
         scol = const.tile([P, 4 * PASSES], F32, name="scol")
         nc.sync.dma_start(out=scol[:].rearrange("p (g t) -> p g t", t=4), in_=W_qkv_scale.rearrange("o (g p t) -> p (o g) t", p=P, t=4))
         for m in range(2):
@@ -296,8 +296,8 @@ def tile_selfattention_pa_kernel(tc, hidden_states, W_qkv_bytes, W_qkv_scale, b_
         rope_at[NT + 1] = [(1, 2, 0, 1), (0, 2, 1, 2)]
         rope_at[NT + 2] = [(1, 2, 1, 2)]
         rope_at[NT + 3] = [(0, 3, 0, 1), (0, 3, 1, 2), (1, 3, 0, 1), (1, 3, 1, 2)]
-        for it in range(NT + d_back + 1):
-            if it < NT and it not in PB_POS:
+        for it in range(-4, NT + d_back + 1):
+            if 0 <= it < NT and it not in PB_POS:
                 stage_tt(it)
             if it == d_q:
                 quantize_x()

@@ -23,8 +23,8 @@ TWO_PI = 6.283185307179586
 
 FLOPS = 2 * SEQ * HID * 3 * NH * P
 
-PB_POS = (0, 10, 20, 30, 40)
-DELTA = 4
+PB_POS = (2, 10, 18, 26, 34, 42)
+DELTA = 2
 
 
 def tile_selfattention_pa_kernel(tc, hidden_states, W_qkv_bytes, W_qkv_scale, b_qkv, out_0, out_1, out_2):
@@ -70,11 +70,11 @@ def tile_selfattention_pa_kernel(tc, hidden_states, W_qkv_bytes, W_qkv_scale, b_
         ident_b = const.tile([P, P], BF16, name="ident_b")
         make_identity(nc, ident_b[:])
 
-        load_w_single(0, 1)
+        load_w_single(0, 0)
         sflat = W_qkv_scale.rearrange("o k -> (o k)")
         nc.sync.dma_start(out=sc[:], in_=sflat.partition_broadcast(P))
         nc.sync.dma_start(out=braw[0:NT, :], in_=b_qkv.rearrange("(i d) -> i d", d=P))
-        load_w_single(0, 0)
+        load_w_single(0, 1)
         scol = const.tile([P, 4 * PASSES], F32, name="scol")
         nc.sync.dma_start(out=scol[:].rearrange("p (g t) -> p g t", t=4), in_=W_qkv_scale.rearrange("o (g p t) -> p (o g) t", p=P, t=4))
         for m in range(2):
@@ -167,7 +167,7 @@ def tile_selfattention_pa_kernel(tc, hidden_states, W_qkv_bytes, W_qkv_scale, b_
         def stage_cast(j, q4):
             if q4 == 0:
                 cbs[j] = pbp.tile([P, HID], BF16, name="cb")
-            cs = slice(512 * q4, 512 * (q4 + 1))
+            cs = slice(1024 * q4, 1024 * (q4 + 1))
             nc.scalar.copy(out=cbs[j][:, cs], in_=wbytes(j)[:, cs].bitcast(FP8))
 
         def stage_tr(j, hf):
@@ -205,8 +205,8 @@ def tile_selfattention_pa_kernel(tc, hidden_states, W_qkv_bytes, W_qkv_scale, b_
         def stage_pb_weave(j, g):
             if g == 0:
                 grp[j] = pbp.tile([P, HID], BF16, name="grpb", align_bytes=64)
-            nc.scalar.copy(out=grp[j][:, 512 * g:512 * (g + 1)].rearrange("p (r t) -> p r t", t=4),
-                           in_=pls[j][:, g, :, :].rearrange("p t r -> p r t"))
+            nc.scalar.copy(out=grp[j][:, 1024 * g:1024 * (g + 1)].rearrange("p (a r t) -> p a r t", a=2, t=4),
+                           in_=pls[j][:, 2 * g:2 * g + 2, :, :].rearrange("p a t r -> p a r t"))
 
         def stage_q(j):
             cd = work.tile([P, PASSES * P], U32, name="codes", align_bytes=64)
@@ -313,9 +313,9 @@ def tile_selfattention_pa_kernel(tc, hidden_states, W_qkv_bytes, W_qkv_scale, b_
                 else:
                     stage_tr_exit(it - d_ex)
             for j0 in PB_POS:
-                if 1 <= j0 - it <= 4:
-                    stage_cast(j0, 4 - (j0 - it))
-                if 4 <= it - j0 <= 7:
+                if 1 <= j0 - it <= 2:
+                    stage_cast(j0, 2 - (j0 - it))
+                if 4 <= it - j0 <= 5:
                     stage_pb_weave(j0, it - j0 - 4)
             if 0 <= it - d_tr < NT:
                 stage_tr(it - d_tr, 0)

@@ -23,7 +23,7 @@ TWO_PI = 6.283185307179586
 
 FLOPS = 2 * SEQ * HID * 3 * NH * P
 
-PB_POS = (2, 10, 18, 26, 34, 42)
+PB_POS = (5, 12, 19, 27, 34, 42)
 DELTA = 2
 
 
@@ -33,7 +33,7 @@ def tile_selfattention_pa_kernel(tc, hidden_states, W_qkv_bytes, W_qkv_scale, b_
     with ExitStack() as ctx:
         const = ctx.enter_context(tc.tile_pool(name="const", bufs=1))
         work = ctx.enter_context(tc.tile_pool(name="work", bufs=3))
-        deep = ctx.enter_context(tc.tile_pool(name="deep", bufs=4))
+        deep = ctx.enter_context(tc.tile_pool(name="deep", bufs=6))
         pbp = ctx.enter_context(tc.tile_pool(name="pbp", bufs=1))
         ogp = ctx.enter_context(tc.tile_pool(name="ogp", bufs=2))
         pst = ctx.enter_context(tc.psum_pool(name="pst", bufs=4))
@@ -72,7 +72,8 @@ def tile_selfattention_pa_kernel(tc, hidden_states, W_qkv_bytes, W_qkv_scale, b_
 
         load_w_single(0, 0)
         sflat = W_qkv_scale.rearrange("o k -> (o k)")
-        nc.sync.dma_start(out=sc[:], in_=sflat.partition_broadcast(P))
+        for q4 in range(4):
+            nc.sync.dma_start(out=sc[:, 512 * q4:512 * (q4 + 1)], in_=sflat[512 * q4:512 * (q4 + 1)].partition_broadcast(P))
         nc.sync.dma_start(out=braw[0:NT, :], in_=b_qkv.rearrange("(i d) -> i d", d=P))
         load_w_single(0, 1)
         scol = const.tile([P, 4 * PASSES], F32, name="scol")
@@ -161,7 +162,11 @@ def tile_selfattention_pa_kernel(tc, hidden_states, W_qkv_bytes, W_qkv_scale, b_
 
         def stage_tt(j):
             t = deep.tile([P, HID], BF16, name="wbf", align_bytes=64)
-            nc.vector.tensor_tensor(out=t[:], in0=wbytes(j).bitcast(FP8), in1=sc[:], op=ALU.mult)
+            nparts = 4 if j == 0 else 1
+            wd = HID // nparts
+            for q4 in range(nparts):
+                cs = slice(wd * q4, wd * (q4 + 1))
+                nc.vector.tensor_tensor(out=t[:, cs], in0=wbytes(j)[:, cs].bitcast(FP8), in1=sc[:, cs], op=ALU.mult)
             wbf[j] = t
 
         def stage_cast(j, q4):
@@ -278,11 +283,11 @@ def tile_selfattention_pa_kernel(tc, hidden_states, W_qkv_bytes, W_qkv_scale, b_
 
         d_tr = 1
         d_ex = 2
-        d_q = 4
-        d_mm = 5
-        d_e1 = 6
-        d_bt = 7
-        d_back = 8
+        d_q = 5
+        d_mm = 6
+        d_e1 = 7
+        d_bt = 8
+        d_back = 9
         rope_at = {}
         qk_count = {}
         for di in range(NT):
@@ -292,10 +297,10 @@ def tile_selfattention_pa_kernel(tc, hidden_states, W_qkv_bytes, W_qkv_scale, b_
                 if qk_count[hg] == 8 and hg < 2:
                     rope_at[di + d_back] = [(0, hg, 0, 2)]
                     rope_at[di + d_back + 1] = [(1, hg, 0, 2)]
-        rope_at[NT] = [(0, 2, 0, 1)]
-        rope_at[NT + 1] = [(1, 2, 0, 1), (0, 2, 1, 2)]
-        rope_at[NT + 2] = [(1, 2, 1, 2)]
-        rope_at[NT + 3] = [(0, 3, 0, 1), (0, 3, 1, 2), (1, 3, 0, 1), (1, 3, 1, 2)]
+        rope_at[NT + 1] = [(0, 2, 0, 1)]
+        rope_at[NT + 2] = [(1, 2, 0, 1), (0, 2, 1, 2)]
+        rope_at[NT + 3] = [(1, 2, 1, 2)]
+        rope_at[NT + 4] = [(0, 3, 0, 1), (0, 3, 1, 2), (1, 3, 0, 1), (1, 3, 1, 2)]
         for it in range(-4, NT + d_back + 1):
             if 0 <= it < NT and it not in PB_POS:
                 stage_tt(it)

@@ -72,8 +72,7 @@ def tile_selfattention_pa_kernel(tc, hidden_states, W_qkv_bytes, W_qkv_scale, b_
 
         load_w_single(0, 0)
         sflat = W_qkv_scale.rearrange("o k -> (o k)")
-        for q4 in range(4):
-            nc.sync.dma_start(out=sc[:, 512 * q4:512 * (q4 + 1)], in_=sflat[512 * q4:512 * (q4 + 1)].partition_broadcast(P))
+        nc.sync.dma_start(out=sc[:], in_=sflat.partition_broadcast(P))
         nc.sync.dma_start(out=braw[0:NT, :], in_=b_qkv.rearrange("(i d) -> i d", d=P))
         load_w_single(0, 1)
         scol = const.tile([P, 4 * PASSES], F32, name="scol")
@@ -162,11 +161,7 @@ def tile_selfattention_pa_kernel(tc, hidden_states, W_qkv_bytes, W_qkv_scale, b_
 
         def stage_tt(j):
             t = deep.tile([P, HID], BF16, name="wbf", align_bytes=64)
-            nparts = 4 if j == 0 else 1
-            wd = HID // nparts
-            for q4 in range(nparts):
-                cs = slice(wd * q4, wd * (q4 + 1))
-                nc.vector.tensor_tensor(out=t[:, cs], in0=wbytes(j)[:, cs].bitcast(FP8), in1=sc[:, cs], op=ALU.mult)
+            nc.vector.tensor_tensor(out=t[:], in0=wbytes(j).bitcast(FP8), in1=sc[:], op=ALU.mult)
             wbf[j] = t
 
         def stage_cast(j, q4):

@@ -65,14 +65,15 @@ def tile_selfattention_pa_kernel(tc, hidden_states, W_qkv_bytes, W_qkv_scale, b_
         zero1 = const.tile([P, 1], F32, name="zero1")
         nc.gpsimd.memset(zero1[:], 0.0)
         nc.gpsimd.memset(braw[:], 0.0)
+        srow = const.tile([P, P], F32, name="srow")
+        nc.gpsimd.memset(srow[:], 0.0)
         ident_f = const.tile([P, P], F32, name="ident_f")
         make_identity(nc, ident_f[:])
         ident_b = const.tile([P, P], BF16, name="ident_b")
         make_identity(nc, ident_b[:])
 
         load_w_single(0, 0)
-        sflat = W_qkv_scale.rearrange("o k -> (o k)")
-        nc.sync.dma_start(out=sc[:], in_=sflat.partition_broadcast(P))
+        nc.sync.dma_start(out=srow[0:16, :], in_=W_qkv_scale.rearrange("o (j n) -> (o j) n", n=P))
         nc.sync.dma_start(out=braw[0:NT, :], in_=b_qkv.rearrange("(i d) -> i d", d=P))
         load_w_single(0, 1)
         scol = const.tile([P, 4 * PASSES], F32, name="scol")
@@ -90,6 +91,15 @@ def tile_selfattention_pa_kernel(tc, hidden_states, W_qkv_bytes, W_qkv_scale, b_
         for j in range(16):
             cj = (1.0 / (10000.0 ** (j / 16.0))) / TWO_PI
             nc.scalar.activation(out=turns[:, :, j:j + 1], in_=pos_f[:].unsqueeze(2), func=ACT.Copy, scale=cj)
+        ps0 = pst.tile([P, 2, 2, P], F32, tag="pt")
+        nc.tensor.transpose(ps0[:, 0, 0, :], srow[:], ident_f[:])
+        scj = const.tile([P, 16], F32, name="scj")
+        nc.scalar.copy(out=scj[:], in_=ps0[:, 0, 0, 0:16])
+        for q4 in range(4):
+            psq = pst.tile([P, 2, 2, P], F32, tag="pt")
+            for jj in range(4):
+                nc.tensor.transpose(psq[:, jj // 2, jj % 2, :], scj[:, 4 * q4 + jj:4 * q4 + jj + 1].to_broadcast([P, P]), ident_f[:])
+            nc.scalar.copy(out=sc[:, 512 * q4:512 * (q4 + 1)], in_=psq[:].rearrange("p a b n -> p (a b n)"))
         tflat = turns[:].rearrange("p m j -> p (m j)")
         n_i = const.tile([P, 32], I32, name="n_i")
         nc.vector.tensor_copy(out=n_i[:], in_=tflat)
@@ -161,7 +171,11 @@ def tile_selfattention_pa_kernel(tc, hidden_states, W_qkv_bytes, W_qkv_scale, b_
 
         def stage_tt(j):
             t = deep.tile([P, HID], BF16, name="wbf", align_bytes=64)
-            nc.vector.tensor_tensor(out=t[:], in0=wbytes(j).bitcast(FP8), in1=sc[:], op=ALU.mult)
+            nparts = 4 if j == 0 else 1
+            wd = HID // nparts
+            for q4 in range(nparts):
+                cs = slice(wd * q4, wd * (q4 + 1))
+                nc.vector.tensor_tensor(out=t[:, cs], in0=wbytes(j)[:, cs].bitcast(FP8), in1=sc[:, cs], op=ALU.mult)
             wbf[j] = t
 
         def stage_cast(j, q4):

@@ -23,8 +23,8 @@ TWO_PI = 6.283185307179586
 
 FLOPS = 2 * SEQ * HID * 3 * NH * P
 
-PB_POS = (5, 12, 19, 27, 34, 42)
-DELTA = 2
+PB_POS = (4, 8, 12, 15, 19, 23, 27, 31, 34, 38, 42)
+DELTA = 3
 
 
 def tile_selfattention_pa_kernel(tc, hidden_states, W_qkv_bytes, W_qkv_scale, b_qkv, out_0, out_1, out_2):
@@ -33,8 +33,9 @@ def tile_selfattention_pa_kernel(tc, hidden_states, W_qkv_bytes, W_qkv_scale, b_
     with ExitStack() as ctx:
         const = ctx.enter_context(tc.tile_pool(name="const", bufs=1))
         work = ctx.enter_context(tc.tile_pool(name="work", bufs=3))
-        deep = ctx.enter_context(tc.tile_pool(name="deep", bufs=6))
-        pbp = ctx.enter_context(tc.tile_pool(name="pbp", bufs=1))
+        deep = ctx.enter_context(tc.tile_pool(name="deep", bufs=4))
+        castp = ctx.enter_context(tc.tile_pool(name="castp", bufs=4))
+        pbp = ctx.enter_context(tc.tile_pool(name="pbp", bufs=2))
         ogp = ctx.enter_context(tc.tile_pool(name="ogp", bufs=2))
         pst = ctx.enter_context(tc.psum_pool(name="pst", bufs=4))
         psa = ctx.enter_context(tc.psum_pool(name="psa", bufs=2))
@@ -55,7 +56,6 @@ def tile_selfattention_pa_kernel(tc, hidden_states, W_qkv_bytes, W_qkv_scale, b_
             for c in range(3):
                 wv[(h, c)] = t[:, c, :]
 
-        sc = const.tile([P, HID], F32, name="sc")
         xraw = [const.tile([P, HID], BF16, name="xraw%d" % m) for m in range(2)]
         xsrc = hidden_states.rearrange("(m p) b k -> p m (b k)", p=P)
         braw = const.tile([P, P], BF16, name="braw")
@@ -65,19 +65,16 @@ def tile_selfattention_pa_kernel(tc, hidden_states, W_qkv_bytes, W_qkv_scale, b_
         zero1 = const.tile([P, 1], F32, name="zero1")
         nc.gpsimd.memset(zero1[:], 0.0)
         nc.gpsimd.memset(braw[:], 0.0)
-        srow = const.tile([P, P], F32, name="srow")
-        nc.gpsimd.memset(srow[:], 0.0)
         ident_f = const.tile([P, P], F32, name="ident_f")
         make_identity(nc, ident_f[:])
         ident_b = const.tile([P, P], BF16, name="ident_b")
         make_identity(nc, ident_b[:])
 
         load_w_single(0, 0)
-        nc.sync.dma_start(out=srow[0:16, :], in_=W_qkv_scale.rearrange("o (j n) -> (o j) n", n=P))
-        nc.sync.dma_start(out=braw[0:NT, :], in_=b_qkv.rearrange("(i d) -> i d", d=P))
-        load_w_single(0, 1)
         scol = const.tile([P, 4 * PASSES], F32, name="scol")
         nc.sync.dma_start(out=scol[:].rearrange("p (g t) -> p g t", t=4), in_=W_qkv_scale.rearrange("o (g p t) -> p (o g) t", p=P, t=4))
+        nc.sync.dma_start(out=braw[0:NT, :], in_=b_qkv.rearrange("(i d) -> i d", d=P))
+        load_w_single(0, 1)
         for m in range(2):
             nc.sync.dma_start(out=xraw[m][:], in_=xsrc[:, m, :])
         load_w_head(1)
@@ -91,15 +88,6 @@ def tile_selfattention_pa_kernel(tc, hidden_states, W_qkv_bytes, W_qkv_scale, b_
         for j in range(16):
             cj = (1.0 / (10000.0 ** (j / 16.0))) / TWO_PI
             nc.scalar.activation(out=turns[:, :, j:j + 1], in_=pos_f[:].unsqueeze(2), func=ACT.Copy, scale=cj)
-        ps0 = pst.tile([P, 2, 2, P], F32, tag="pt")
-        nc.tensor.transpose(ps0[:, 0, 0, :], srow[:], ident_f[:])
-        scj = const.tile([P, 16], F32, name="scj")
-        nc.scalar.copy(out=scj[:], in_=ps0[:, 0, 0, 0:16])
-        for q4 in range(4):
-            psq = pst.tile([P, 2, 2, P], F32, tag="pt")
-            for jj in range(4):
-                nc.tensor.transpose(psq[:, jj // 2, jj % 2, :], scj[:, 4 * q4 + jj:4 * q4 + jj + 1].to_broadcast([P, P]), ident_f[:])
-            nc.scalar.copy(out=sc[:, 512 * q4:512 * (q4 + 1)], in_=psq[:].rearrange("p a b n -> p (a b n)"))
         tflat = turns[:].rearrange("p m j -> p (m j)")
         n_i = const.tile([P, 32], I32, name="n_i")
         nc.vector.tensor_copy(out=n_i[:], in_=tflat)
@@ -116,19 +104,24 @@ def tile_selfattention_pa_kernel(tc, hidden_states, W_qkv_bytes, W_qkv_scale, b_
                                        op0=ALU.is_gt, op1=ALU.subtract)
         cosT = const.tile([P, 2, 32], F32, name="cosT")
         sinT = const.tile([P, 2, 32], F32, name="sinT")
-        nc.scalar.activation(out=cosT[:, :, 0:16], in_=wr2[:, 1, :, :], func=ACT.Sin, scale=TWO_PI)
-        nc.scalar.activation(out=cosT[:, :, 16:32], in_=wr2[:, 1, :, :], func=ACT.Sin, scale=TWO_PI)
-        nc.scalar.activation(out=sinT[:, :, 0:16], in_=wr2[:, 0, :, :], func=ACT.Sin, scale=-TWO_PI)
-        nc.scalar.activation(out=sinT[:, :, 16:32], in_=wr2[:, 0, :, :], func=ACT.Sin, scale=TWO_PI)
 
-        pbias = psb.tile([P, P], BF16, tag="pb")
-        nc.tensor.transpose(pbias[:], braw[:], ident_b[:])
+        def make_sins():
+            nc.scalar.activation(out=cosT[:, :, 0:16], in_=wr2[:, 1, :, :], func=ACT.Sin, scale=TWO_PI)
+            nc.scalar.activation(out=cosT[:, :, 16:32], in_=wr2[:, 1, :, :], func=ACT.Sin, scale=TWO_PI)
+            nc.scalar.activation(out=sinT[:, :, 0:16], in_=wr2[:, 0, :, :], func=ACT.Sin, scale=-TWO_PI)
+            nc.scalar.activation(out=sinT[:, :, 16:32], in_=wr2[:, 0, :, :], func=ACT.Sin, scale=TWO_PI)
+
         bias = const.tile([P, NT], F32, name="bias")
-        nc.scalar.copy(out=bias[:], in_=pbias[:, 0:NT])
+
+        def make_bias():
+            pbias = psb.tile([P, P], BF16, tag="pb")
+            nc.tensor.transpose(pbias[:], braw[:], ident_b[:])
+            nc.scalar.copy(out=bias[:], in_=pbias[:, 0:NT])
 
         xg = const.tile([P, PASSES * SEQ * 4], BF16, name="xg", align_bytes=64)
         xgw = xg[:].bitcast(F32).rearrange("p (g s u) -> p g s u", g=PASSES, u=2)
-        for m in range(2):
+
+        def turn_x(m):
             xw = xraw[m][:].bitcast(F32)
             for hf in range(2):
                 pt = pst.tile([P, 2, 2, P], F32, tag="pt")
@@ -137,6 +130,7 @@ def tile_selfattention_pa_kernel(tc, hidden_states, W_qkv_bytes, W_qkv_scale, b_
                     for u in range(2):
                         nc.tensor.transpose(pt[:, gg, u, :], xw[:, 256 * g + u:256 * (g + 1):2], ident_f[:])
                 nc.scalar.copy(out=xgw[:, 2 * hf:2 * hf + 2, m * P:(m + 1) * P, :], in_=pt[:].rearrange("p g u r -> p g r u"))
+
         xcodes = const.tile([P, PASSES * SEQ], U32, name="xcodes", align_bytes=64)
         xscl = const.tile([P, PASSES * SEQ], U8, name="xscl", align_bytes=64)
 
@@ -169,42 +163,31 @@ def tile_selfattention_pa_kernel(tc, hidden_states, W_qkv_bytes, W_qkv_scale, b_
             hg, hh, c = order[j]
             return wv[(4 * hg + hh, c)]
 
-        def stage_tt(j):
-            t = deep.tile([P, HID], BF16, name="wbf", align_bytes=64)
+        def stage_cast(j):
+            t = castp.tile([P, HID], BF16, name="cb", align_bytes=64)
             nparts = 4 if j == 0 else 1
             wd = HID // nparts
             for q4 in range(nparts):
-                cs = slice(wd * q4, wd * (q4 + 1))
-                nc.vector.tensor_tensor(out=t[:, cs], in0=wbytes(j)[:, cs].bitcast(FP8), in1=sc[:, cs], op=ALU.mult)
-            wbf[j] = t
-
-        def stage_cast(j, q4):
-            if q4 == 0:
-                cbs[j] = pbp.tile([P, HID], BF16, name="cb")
-            cs = slice(1024 * q4, 1024 * (q4 + 1))
-            nc.scalar.copy(out=cbs[j][:, cs], in_=wbytes(j)[:, cs].bitcast(FP8))
+                cs = slice(wd * q4, wd * q4 + wd)
+                nc.scalar.copy(out=t[:, cs], in_=wbytes(j)[:, cs].bitcast(FP8))
+            cbs[j] = t
 
         def stage_tr(j, hf):
-            if j in PB_POS:
-                pt = pst.tile([P, 2, 4, P], BF16, tag="pt")
-                for gg in range(2):
-                    g = 2 * hf + gg
-                    for t in range(4):
-                        nc.tensor.transpose(pt[:, gg, t, :], cbs[j][:, 512 * g + t:512 * (g + 1):4], ident_b[:])
-            else:
-                raw = wbf[j][:].bitcast(F32)
-                pt = pst.tile([P, 2, 2, P], F32, tag="pt")
-                for gg in range(2):
-                    g = 2 * hf + gg
-                    for u in range(2):
-                        nc.tensor.transpose(pt[:, gg, u, :], raw[:, 256 * g + u:256 * (g + 1):2], ident_f[:])
-            ptt[(j, hf)] = pt
+            raw = cbs[j][:].bitcast(F32)
+            pt = pst.tile([P, 2, 2, P], F32, tag="pt")
+            for gg in range(2):
+                g = 2 * hf + gg
+                for u in range(2):
+                    nc.tensor.transpose(pt[:, u, gg, :], raw[:, 256 * g + u:256 * (g + 1):2], ident_f[:])
+            ptt[(j, hf)] = pt[:].rearrange("p u g r -> p (u g r)").bitcast(BF16).rearrange("p (u g r e) -> p g r u e", g=2, u=2, e=2)
 
-        def stage_tr_exit(j):
+        def stage_tt(j):
             t = deep.tile([P, HID], BF16, name="grp", align_bytes=64)
-            tw = t[:].bitcast(F32).rearrange("p (g r u) -> p g r u", g=PASSES, u=2)
             for hf in range(2):
-                nc.scalar.copy(out=tw[:, 2 * hf:2 * hf + 2, :, :], in_=ptt[(j, hf)][:].rearrange("p g u r -> p g r u"))
+                nc.vector.tensor_tensor(out=t[:, 1024 * hf:1024 * (hf + 1)].rearrange("p (g r u e) -> p g r u e", g=2, u=2, e=2),
+                                        in0=ptt[(j, hf)],
+                                        in1=scol[:, 8 * hf:8 * hf + 8].rearrange("p (g u e) -> p g u e", g=2, u=2).unsqueeze(2).to_broadcast([P, 2, P, 2, 2]),
+                                        op=ALU.mult)
             grp[j] = t
 
         def stage_pb_exit(j, hf):
@@ -213,14 +196,16 @@ def tile_selfattention_pa_kernel(tc, hidden_states, W_qkv_bytes, W_qkv_scale, b_
             for gg in range(2):
                 g = 2 * hf + gg
                 for t in range(4):
-                    nc.scalar.activation(out=pls[j][:, g, t, :], in_=ptt[(j, hf)][:, gg, t, :], func=ACT.Copy,
+                    nc.scalar.activation(out=pls[j][:, g, t, :], in_=ptt[(j, hf)][:, gg, :, t // 2, t % 2], func=ACT.Copy,
                                          scale=scol[:, 4 * g + t:4 * g + t + 1])
 
-        def stage_pb_weave(j, g):
-            if g == 0:
+        def stage_pb_weave(j, hf):
+            if hf == 0:
                 grp[j] = pbp.tile([P, HID], BF16, name="grpb", align_bytes=64)
-            nc.scalar.copy(out=grp[j][:, 1024 * g:1024 * (g + 1)].rearrange("p (a r t) -> p a r t", a=2, t=4),
-                           in_=pls[j][:, 2 * g:2 * g + 2, :, :].rearrange("p a t r -> p a r t"))
+            for g in range(2 * hf, 2 * hf + 2):
+                nc.gpsimd.tensor_scalar(out=grp[j][:, 512 * g:512 * (g + 1)].rearrange("p (r t) -> p r t", t=4),
+                                        in0=pls[j][:, g, :, :].rearrange("p t r -> p r t"),
+                                        scalar1=1.0, scalar2=0.0, op0=ALU.mult, op1=ALU.add)
 
         def stage_q(j):
             cd = work.tile([P, PASSES * P], U32, name="codes", align_bytes=64)
@@ -291,46 +276,38 @@ def tile_selfattention_pa_kernel(tc, hidden_states, W_qkv_bytes, W_qkv_scale, b_
                 nc.sync.dma_start(out=ov[c][:, :, 4 * hg:4 * hg + 4, :], in_=og[hg][:, :, 4 * c:4 * c + 4, :])
 
         d_tr = 1
-        d_ex = 2
-        d_q = 5
-        d_mm = 6
-        d_e1 = 7
-        d_bt = 8
-        d_back = 9
+        d_tt = 2
+        d_q = 4
+        d_mm = 5
+        d_e1 = 6
+        d_bt = 7
+        d_back = 8
         rope_at = {}
         qk_count = {}
         for di in range(NT):
             hg, hh, c = order[down[di]]
             if c < 2:
                 qk_count[hg] = qk_count.get(hg, 0) + 1
-                if qk_count[hg] == 8 and hg < 2:
-                    rope_at[di + d_back] = [(0, hg, 0, 2)]
-                    rope_at[di + d_back + 1] = [(1, hg, 0, 2)]
-        rope_at[NT + 1] = [(0, 2, 0, 1)]
-        rope_at[NT + 2] = [(1, 2, 0, 1), (0, 2, 1, 2)]
-        rope_at[NT + 3] = [(1, 2, 1, 2)]
-        rope_at[NT + 4] = [(0, 3, 0, 1), (0, 3, 1, 2), (1, 3, 0, 1), (1, 3, 1, 2)]
-        for it in range(-4, NT + d_back + 1):
-            if 0 <= it < NT and it not in PB_POS:
-                stage_tt(it)
-            if it == d_q:
-                quantize_x()
+                if qk_count[hg] == 8 and hg < 3:
+                    rope_at[di + d_back + 1] = [(0, hg, 0, 2)]
+                    rope_at[di + d_back + 2] = [(1, hg, 0, 2)]
+        rope_at[NT + d_q] = [(0, 3, 0, 1), (0, 3, 1, 2), (1, 3, 0, 1), (1, 3, 1, 2)]
+        for it in range(NT + d_back + 1):
+            if 0 <= it - d_tt < NT and it - d_tt not in PB_POS:
+                stage_tt(it - d_tt)
             if 0 <= it - d_e1 < NT:
                 stage_mm_exit(down[it - d_e1])
             if 0 <= it - d_back < NT:
                 stage_back_exit(down[it - d_back])
-            if it - d_ex - 1 in PB_POS:
-                stage_pb_exit(it - d_ex - 1, 1)
-            if 0 <= it - d_ex < NT:
-                if it - d_ex in PB_POS:
-                    stage_pb_exit(it - d_ex, 0)
-                else:
-                    stage_tr_exit(it - d_ex)
-            for j0 in PB_POS:
-                if 1 <= j0 - it <= 2:
-                    stage_cast(j0, 2 - (j0 - it))
-                if 4 <= it - j0 <= 5:
-                    stage_pb_weave(j0, it - j0 - 4)
+            if it < NT:
+                stage_cast(it)
+            if it == 1:
+                make_sins()
+            for hf in range(2):
+                if it - d_tt - hf in PB_POS:
+                    stage_pb_exit(it - d_tt - hf, hf)
+                if it - d_tt - 1 - hf in PB_POS:
+                    stage_pb_weave(it - d_tt - 1 - hf, hf)
             if 0 <= it - d_tr < NT:
                 stage_tr(it - d_tr, 0)
             if 0 <= it - d_mm < NT:
@@ -339,6 +316,13 @@ def tile_selfattention_pa_kernel(tc, hidden_states, W_qkv_bytes, W_qkv_scale, b_
                 stage_tr(it - d_tr, 1)
             if 0 <= it - d_bt < NT:
                 stage_back(down[it - d_bt])
+            if it == 2:
+                turn_x(0)
+            if it == 3:
+                make_bias()
+                turn_x(1)
+            if it == d_q:
+                quantize_x()
             if 0 <= it - d_q < NT:
                 stage_q(down[it - d_q])
             for act, hg, c0, c1 in rope_at.get(it, []):

@@ -23,8 +23,8 @@ TWO_PI = 6.283185307179586
 
 FLOPS = 2 * SEQ * HID * 3 * NH * P
 
-PB_POS = (4, 8, 12, 15, 19, 23, 27, 31, 34, 38, 42)
-DELTA = 3
+S_HALVES = range(3, NT - 1, 2)
+LAST_BACK_MATMUL = 42
 
 
 def tile_selfattention_pa_kernel(tc, hidden_states, W_qkv_bytes, W_qkv_scale, b_qkv, out_0, out_1, out_2):
@@ -33,13 +33,12 @@ def tile_selfattention_pa_kernel(tc, hidden_states, W_qkv_bytes, W_qkv_scale, b_
     with ExitStack() as ctx:
         const = ctx.enter_context(tc.tile_pool(name="const", bufs=1))
         work = ctx.enter_context(tc.tile_pool(name="work", bufs=3))
-        deep = ctx.enter_context(tc.tile_pool(name="deep", bufs=4))
-        castp = ctx.enter_context(tc.tile_pool(name="castp", bufs=4))
-        pbp = ctx.enter_context(tc.tile_pool(name="pbp", bufs=2))
+        deep = ctx.enter_context(tc.tile_pool(name="deep", bufs=5))
+        castp = ctx.enter_context(tc.tile_pool(name="castp", bufs=6))
+        pbp = ctx.enter_context(tc.tile_pool(name="pbp", bufs=3))
         ogp = ctx.enter_context(tc.tile_pool(name="ogp", bufs=2))
-        pst = ctx.enter_context(tc.psum_pool(name="pst", bufs=4))
-        psa = ctx.enter_context(tc.psum_pool(name="psa", bufs=2))
-        psb = ctx.enter_context(tc.psum_pool(name="psb", bufs=2))
+        pst = ctx.enter_context(tc.psum_pool(name="pst", bufs=5))
+        psa = ctx.enter_context(tc.psum_pool(name="psa", bufs=3))
         ctx.enter_context(tc.manual_schedule())
 
         wrows = W_qkv_bytes.rearrange("(i p) k -> p i k", p=P)
@@ -114,7 +113,7 @@ def tile_selfattention_pa_kernel(tc, hidden_states, W_qkv_bytes, W_qkv_scale, b_
         bias = const.tile([P, NT], F32, name="bias")
 
         def make_bias():
-            pbias = psb.tile([P, P], BF16, tag="pb")
+            pbias = psa.tile([P, P], BF16, tag="acc")
             nc.tensor.transpose(pbias[:], braw[:], ident_b[:])
             nc.scalar.copy(out=bias[:], in_=pbias[:, 0:NT])
 
@@ -148,13 +147,6 @@ def tile_selfattention_pa_kernel(tc, hidden_states, W_qkv_bytes, W_qkv_scale, b_
                     order.append((hg, hh, 1))
                 else:
                     order.append((hg, hh, 2))
-        down = []
-        for idx in range(NT):
-            if idx not in PB_POS:
-                down.append(idx)
-            if idx - DELTA in PB_POS:
-                down.append(idx - DELTA)
-        assert len(down) == NT
         wbf, cbs, pls, grp, codes, scl, usb, og = {}, {}, {}, {}, {}, {}, {}, {}
         ptt, accs, pbs = {}, {}, {}
         ov = [o.rearrange("(m p) b h d -> p m (b h) d", p=P) for o in outs]
@@ -165,11 +157,15 @@ def tile_selfattention_pa_kernel(tc, hidden_states, W_qkv_bytes, W_qkv_scale, b_
 
         def stage_cast(j):
             t = castp.tile([P, HID], BF16, name="cb", align_bytes=64)
+            ns = HID // 2 if j in S_HALVES else HID
             nparts = 4 if j == 0 else 1
-            wd = HID // nparts
-            for q4 in range(nparts):
-                cs = slice(wd * q4, wd * q4 + wd)
+            wd = ns // nparts
+            for c0 in range(0, ns, wd):
+                cs = slice(c0, c0 + wd)
                 nc.scalar.copy(out=t[:, cs], in_=wbytes(j)[:, cs].bitcast(FP8))
+            for c0 in range(ns, HID, 512):
+                cs = slice(c0, c0 + 512)
+                nc.gpsimd.tensor_copy(out=t[:, cs], in_=wbytes(j)[:, cs].bitcast(FP8))
             cbs[j] = t
 
         def stage_tr(j, hf):
@@ -183,28 +179,26 @@ def tile_selfattention_pa_kernel(tc, hidden_states, W_qkv_bytes, W_qkv_scale, b_
 
         def stage_tt(j):
             t = deep.tile([P, HID], BF16, name="grp", align_bytes=64)
-            for hf in range(2):
+            for hf in range(1 if j in S_HALVES else 2):
                 nc.vector.tensor_tensor(out=t[:, 1024 * hf:1024 * (hf + 1)].rearrange("p (g r u e) -> p g r u e", g=2, u=2, e=2),
                                         in0=ptt[(j, hf)],
                                         in1=scol[:, 8 * hf:8 * hf + 8].rearrange("p (g u e) -> p g u e", g=2, u=2).unsqueeze(2).to_broadcast([P, 2, P, 2, 2]),
                                         op=ALU.mult)
             grp[j] = t
 
-        def stage_pb_exit(j, hf):
-            if hf == 0:
-                pls[j] = pbp.tile([P, PASSES, 4, P], BF16, name="pl")
+        def stage_s_scale(j):
+            pls[j] = pbp.tile([P, 2, 4, P], BF16, name="pl")
             for gg in range(2):
-                g = 2 * hf + gg
+                g = 2 + gg
                 for t in range(4):
-                    nc.scalar.activation(out=pls[j][:, g, t, :], in_=ptt[(j, hf)][:, gg, :, t // 2, t % 2], func=ACT.Copy,
+                    nc.scalar.activation(out=pls[j][:, gg, t, :], in_=ptt[(j, 1)][:, gg, :, t // 2, t % 2], func=ACT.Copy,
                                          scale=scol[:, 4 * g + t:4 * g + t + 1])
 
-        def stage_pb_weave(j, hf):
-            if hf == 0:
-                grp[j] = pbp.tile([P, HID], BF16, name="grpb", align_bytes=64)
-            for g in range(2 * hf, 2 * hf + 2):
-                nc.gpsimd.tensor_scalar(out=grp[j][:, 512 * g:512 * (g + 1)].rearrange("p (r t) -> p r t", t=4),
-                                        in0=pls[j][:, g, :, :].rearrange("p t r -> p r t"),
+        def stage_weave(j):
+            for gg in range(2):
+                c0 = 512 * (2 + gg)
+                nc.gpsimd.tensor_scalar(out=grp[j][:, c0:c0 + 512].rearrange("p (r t) -> p r t", t=4),
+                                        in0=pls[j][:, gg, :, :].rearrange("p t r -> p r t"),
                                         scalar1=1.0, scalar2=0.0, op0=ALU.mult, op1=ALU.add)
 
         def stage_q(j):
@@ -233,9 +227,12 @@ def tile_selfattention_pa_kernel(tc, hidden_states, W_qkv_bytes, W_qkv_scale, b_
             usb[j] = u
 
         def stage_back(j):
-            pb = psb.tile([P, 2, P], F32, tag="pb")
+            pb = psa.tile([P, 2, P], F32, tag="acc")
             for m in range(2):
-                nc.tensor.matmul(pb[:, m, :], lhsT=usb[j][:, m * P:(m + 1) * P], rhs=ident_f[:], start=True, stop=True)
+                if j < LAST_BACK_MATMUL:
+                    nc.tensor.matmul(pb[:, m, :], lhsT=usb[j][:, m * P:(m + 1) * P], rhs=ident_f[:], start=True, stop=True)
+                else:
+                    nc.tensor.transpose(pb[:, m, :], usb[j][:, m * P:(m + 1) * P], ident_f[:])
             pbs[j] = pb
 
         v_count = {}
@@ -278,44 +275,36 @@ def tile_selfattention_pa_kernel(tc, hidden_states, W_qkv_bytes, W_qkv_scale, b_
         d_tr = 1
         d_tt = 2
         d_q = 4
-        d_mm = 5
-        d_e1 = 6
-        d_bt = 7
-        d_back = 8
+        d_mm = d_q + 1
+        d_bt = d_q + 3
+        d_back = d_q + 4
         rope_at = {}
-        qk_count = {}
-        for di in range(NT):
-            hg, hh, c = order[down[di]]
-            if c < 2:
-                qk_count[hg] = qk_count.get(hg, 0) + 1
-                if qk_count[hg] == 8 and hg < 3:
-                    rope_at[di + d_back + 1] = [(0, hg, 0, 2)]
-                    rope_at[di + d_back + 2] = [(1, hg, 0, 2)]
-        rope_at[NT + d_q] = [(0, 3, 0, 1), (0, 3, 1, 2), (1, 3, 0, 1), (1, 3, 1, 2)]
-        for it in range(NT + d_back + 1):
-            if 0 <= it - d_tt < NT and it - d_tt not in PB_POS:
+        for hg, last in ((0, 7), (1, 19), (2, 31)):
+            rope_at[last + d_back + 1] = [(0, hg, 0, 2)]
+            rope_at[last + d_back + 2] = [(1, hg, 0, 2)]
+        rope_at[NT + d_q - 1] = [(0, 3, 0, 1), (0, 3, 1, 2), (1, 3, 0, 1), (1, 3, 1, 2)]
+        for it in range(NT + d_back):
+            if 0 <= it - d_tt < NT:
                 stage_tt(it - d_tt)
-            if 0 <= it - d_e1 < NT:
-                stage_mm_exit(down[it - d_e1])
             if 0 <= it - d_back < NT:
-                stage_back_exit(down[it - d_back])
+                stage_back_exit(it - d_back)
+            if it - d_tt in S_HALVES:
+                stage_s_scale(it - d_tt)
             if it < NT:
                 stage_cast(it)
+            if it - d_tt in S_HALVES:
+                stage_weave(it - d_tt)
             if it == 1:
                 make_sins()
-            for hf in range(2):
-                if it - d_tt - hf in PB_POS:
-                    stage_pb_exit(it - d_tt - hf, hf)
-                if it - d_tt - 1 - hf in PB_POS:
-                    stage_pb_weave(it - d_tt - 1 - hf, hf)
             if 0 <= it - d_tr < NT:
                 stage_tr(it - d_tr, 0)
             if 0 <= it - d_mm < NT:
-                stage_mm(down[it - d_mm])
+                stage_mm(it - d_mm)
+                stage_mm_exit(it - d_mm)
+            if 0 <= it - d_bt < NT:
+                stage_back(it - d_bt)
             if 0 <= it - d_tr < NT:
                 stage_tr(it - d_tr, 1)
-            if 0 <= it - d_bt < NT:
-                stage_back(down[it - d_bt])
             if it == 2:
                 turn_x(0)
             if it == 3:
@@ -324,7 +313,7 @@ def tile_selfattention_pa_kernel(tc, hidden_states, W_qkv_bytes, W_qkv_scale, b_
             if it == d_q:
                 quantize_x()
             if 0 <= it - d_q < NT:
-                stage_q(down[it - d_q])
+                stage_q(it - d_q)
             for act, hg, c0, c1 in rope_at.get(it, []):
                 if act == 0:
                     rope_mul(hg, c0, c1)

@@ -33,8 +33,9 @@ def tile_selfattention_pa_kernel(tc, hidden_states, W_qkv_bytes, W_qkv_scale, b_
     with ExitStack() as ctx:
         const = ctx.enter_context(tc.tile_pool(name="const", bufs=1))
         work = ctx.enter_context(tc.tile_pool(name="work", bufs=3))
-        deep = ctx.enter_context(tc.tile_pool(name="deep", bufs=5))
-        castp = ctx.enter_context(tc.tile_pool(name="castp", bufs=6))
+        deep = ctx.enter_context(tc.tile_pool(name="deep", bufs=3))
+        castp = ctx.enter_context(tc.tile_pool(name="castp", bufs=5))
+        usbp = ctx.enter_context(tc.tile_pool(name="usbp", bufs=3))
         pbp = ctx.enter_context(tc.tile_pool(name="pbp", bufs=3))
         ogp = ctx.enter_context(tc.tile_pool(name="ogp", bufs=2))
         pst = ctx.enter_context(tc.psum_pool(name="pst", bufs=5))
@@ -69,6 +70,15 @@ def tile_selfattention_pa_kernel(tc, hidden_states, W_qkv_bytes, W_qkv_scale, b_
         ident_b = const.tile([P, P], BF16, name="ident_b")
         make_identity(nc, ident_b[:])
 
+        ones = const.tile([P, P], F32, name="ones")
+        nc.vector.memset(ones[:], 1.0)
+
+        def keep_awake(n):
+            for i in range(n):
+                junk = psa.tile([P, P], F32, tag="acc")
+                nc.tensor.matmul(junk[:], lhsT=ones[:], rhs=ones[:], start=True, stop=True)
+
+        keep_awake(7)
         load_w_single(0, 0)
         scol = const.tile([P, 4 * PASSES], F32, name="scol")
         nc.sync.dma_start(out=scol[:].rearrange("p (g t) -> p g t", t=4), in_=W_qkv_scale.rearrange("o (g p t) -> p (o g) t", p=P, t=4))
@@ -80,6 +90,11 @@ def tile_selfattention_pa_kernel(tc, hidden_states, W_qkv_bytes, W_qkv_scale, b_
         load_w_single(0, 2)
         for h in range(2, NH):
             load_w_head(h)
+
+        sct = const.tile([P, HID], F32, name="sct")
+        for g in range(PASSES):
+            nc.gpsimd.tensor_copy(out=sct[:, 512 * g:512 * (g + 1)].rearrange("p (r t) -> p r t", t=4),
+                                  in_=scol[:, 4 * g:4 * g + 4].unsqueeze(1).to_broadcast([P, P, 4]))
 
         warm = const.tile([P, 1], F32, name="warm")
         nc.scalar.activation(out=warm[:], in_=zero1[:], func=ACT.Sin)
@@ -148,7 +163,7 @@ def tile_selfattention_pa_kernel(tc, hidden_states, W_qkv_bytes, W_qkv_scale, b_
                 else:
                     order.append((hg, hh, 2))
         wbf, cbs, pls, grp, codes, scl, usb, og = {}, {}, {}, {}, {}, {}, {}, {}
-        ptt, accs, pbs = {}, {}, {}
+        ptt, accs, pbs, pairs = {}, {}, {}, {}
         ov = [o.rearrange("(m p) b h d -> p m (b h) d", p=P) for o in outs]
 
         def wbytes(j):
@@ -157,7 +172,7 @@ def tile_selfattention_pa_kernel(tc, hidden_states, W_qkv_bytes, W_qkv_scale, b_
 
         def stage_cast(j):
             t = castp.tile([P, HID], BF16, name="cb", align_bytes=64)
-            ns = HID // 2 if j in S_HALVES else HID
+            ns = HID
             nparts = 4 if j == 0 else 1
             wd = ns // nparts
             for c0 in range(0, ns, wd):
@@ -178,13 +193,15 @@ def tile_selfattention_pa_kernel(tc, hidden_states, W_qkv_bytes, W_qkv_scale, b_
             ptt[(j, hf)] = pt[:].rearrange("p u g r -> p (u g r)").bitcast(BF16).rearrange("p (u g r e) -> p g r u e", g=2, u=2, e=2)
 
         def stage_tt(j):
-            t = deep.tile([P, HID], BF16, name="grp", align_bytes=64)
+            if j % 2 == 0:
+                pair = deep.tile([P, 2 * HID], BF16, name="grp", align_bytes=64)
+                grp[j], grp[j + 1] = pair[:, 0:HID], pair[:, HID:2 * HID]
+                pairs[j] = pair
             for hf in range(1 if j in S_HALVES else 2):
-                nc.vector.tensor_tensor(out=t[:, 1024 * hf:1024 * (hf + 1)].rearrange("p (g r u e) -> p g r u e", g=2, u=2, e=2),
+                nc.vector.tensor_tensor(out=grp[j][:, 1024 * hf:1024 * (hf + 1)].rearrange("p (g r u e) -> p g r u e", g=2, u=2, e=2),
                                         in0=ptt[(j, hf)],
-                                        in1=scol[:, 8 * hf:8 * hf + 8].rearrange("p (g u e) -> p g u e", g=2, u=2).unsqueeze(2).to_broadcast([P, 2, P, 2, 2]),
+                                        in1=sct[:, 1024 * hf:1024 * (hf + 1)].rearrange("p (g r u e) -> p g r u e", g=2, u=2, e=2),
                                         op=ALU.mult)
-            grp[j] = t
 
         def stage_s_scale(j):
             pls[j] = pbp.tile([P, 2, 4, P], BF16, name="pl")
@@ -202,11 +219,17 @@ def tile_selfattention_pa_kernel(tc, hidden_states, W_qkv_bytes, W_qkv_scale, b_
                                         scalar1=1.0, scalar2=0.0, op0=ALU.mult, op1=ALU.add)
 
         def stage_q(j):
-            cd = work.tile([P, PASSES * P], U32, name="codes", align_bytes=64)
-            sl = work.tile([P, PASSES * P], U8, name="scl", align_bytes=64)
-            nc.vector.quantize_mx(out=cd[:].bitcast(FP8X4), scales=sl[:], in_=grp[j][:])
-            codes[j] = cd
-            scl[j] = sl
+            cd = work.tile([P, 2 * PASSES * P], U32, name="codes", align_bytes=64)
+            sl = work.tile([P, 2 * PASSES * P], U8, name="scl", align_bytes=64)
+            if j < NT - 2:
+                nc.vector.quantize_mx(out=cd[:].bitcast(FP8X4), scales=sl[:], in_=pairs[j][:])
+            else:
+                for i in range(2):
+                    nc.vector.quantize_mx(out=cd[:, 512 * i:512 * (i + 1)].bitcast(FP8X4), scales=sl[:, 512 * i:512 * (i + 1)],
+                                          in_=grp[j + i])
+            for i in range(2):
+                codes[j + i] = cd[:, 512 * i:512 * (i + 1)]
+                scl[j + i] = sl[:, 512 * i:512 * (i + 1)]
 
         def stage_mm(j):
             acc = psa.tile([P, SEQ], F32, tag="acc")
@@ -221,7 +244,7 @@ def tile_selfattention_pa_kernel(tc, hidden_states, W_qkv_bytes, W_qkv_scale, b_
 
         def stage_mm_exit(j):
             hg, hh, c = order[j]
-            u = work.tile([P, SEQ], F32, name="usb")
+            u = usbp.tile([P, SEQ], F32, name="usb")
             i = 3 * (4 * hg + hh) + c
             nc.scalar.activation(out=u[:], in_=accs[j][:], func=ACT.Identity, bias=bias[:, i:i + 1], scale=1.0)
             usb[j] = u
@@ -253,36 +276,38 @@ def tile_selfattention_pa_kernel(tc, hidden_states, W_qkv_bytes, W_qkv_scale, b_
         rtmp = {}
 
         def rope_mul(hg, c0, c1):
+            eng = nc.gpsimd
             o = og[hg]
             n = 4 * (c1 - c0)
             ts = slice(4 * c0, 4 * c1)
             ra = ogp.tile([P, 2, n, 32], F32, name="ra")
             rb = ogp.tile([P, 2, n, 32], F32, name="rb")
-            nc.vector.tensor_tensor(out=rb[:, :, :, 0:16], in0=o[:, :, ts, 16:32],
+            eng.tensor_tensor(out=rb[:, :, :, 0:16], in0=o[:, :, ts, 16:32],
                                     in1=sinT[:, :, 0:16].unsqueeze(2).to_broadcast([P, 2, n, 16]), op=ALU.mult)
-            nc.vector.tensor_tensor(out=rb[:, :, :, 16:32], in0=o[:, :, ts, 0:16],
+            eng.tensor_tensor(out=rb[:, :, :, 16:32], in0=o[:, :, ts, 0:16],
                                     in1=sinT[:, :, 16:32].unsqueeze(2).to_broadcast([P, 2, n, 16]), op=ALU.mult)
-            nc.vector.tensor_tensor(out=ra[:], in0=o[:, :, ts, 0:32],
+            eng.tensor_tensor(out=ra[:], in0=o[:, :, ts, 0:32],
                                     in1=cosT[:].unsqueeze(2).to_broadcast([P, 2, n, 32]), op=ALU.mult)
             rtmp[(hg, c0)] = (ra, rb)
 
         def rope_add_store(hg, c0, c1):
+            eng = nc.gpsimd
             ra, rb = rtmp[(hg, c0)]
-            nc.vector.tensor_tensor(out=og[hg][:, :, 4 * c0:4 * c1, 0:32], in0=ra[:], in1=rb[:], op=ALU.add)
+            eng.tensor_tensor(out=og[hg][:, :, 4 * c0:4 * c1, 0:32], in0=ra[:], in1=rb[:], op=ALU.add)
             for c in range(c0, c1):
                 nc.sync.dma_start(out=ov[c][:, :, 4 * hg:4 * hg + 4, :], in_=og[hg][:, :, 4 * c:4 * c + 4, :])
 
-        d_tr = 1
-        d_tt = 2
+        d_tr = 2
+        d_tt = 3
         d_q = 4
-        d_mm = d_q + 1
-        d_bt = d_q + 3
-        d_back = d_q + 4
+        d_mm = 7
+        d_e1 = 7
+        d_bt = 9
+        d_back = 10
         rope_at = {}
-        for hg, last in ((0, 7), (1, 19), (2, 31)):
+        for hg, last in ((0, 7), (1, 19), (2, 31), (3, 39)):
             rope_at[last + d_back + 1] = [(0, hg, 0, 2)]
             rope_at[last + d_back + 2] = [(1, hg, 0, 2)]
-        rope_at[NT + d_q - 1] = [(0, 3, 0, 1), (0, 3, 1, 2), (1, 3, 0, 1), (1, 3, 1, 2)]
         for it in range(NT + d_back):
             if 0 <= it - d_tt < NT:
                 stage_tt(it - d_tt)
@@ -290,30 +315,34 @@ def tile_selfattention_pa_kernel(tc, hidden_states, W_qkv_bytes, W_qkv_scale, b_
                 stage_back_exit(it - d_back)
             if it - d_tt in S_HALVES:
                 stage_s_scale(it - d_tt)
+                stage_weave(it - d_tt)
             if it < NT:
                 stage_cast(it)
-            if it - d_tt in S_HALVES:
-                stage_weave(it - d_tt)
             if it == 1:
                 make_sins()
             if 0 <= it - d_tr < NT:
                 stage_tr(it - d_tr, 0)
             if 0 <= it - d_mm < NT:
                 stage_mm(it - d_mm)
-                stage_mm_exit(it - d_mm)
+            if 0 <= it - d_e1 < NT:
+                stage_mm_exit(it - d_e1)
             if 0 <= it - d_bt < NT:
                 stage_back(it - d_bt)
+            if d_tr <= it < d_mm:
+                keep_awake(2)
             if 0 <= it - d_tr < NT:
                 stage_tr(it - d_tr, 1)
-            if it == 2:
+            if d_tr <= it < d_mm:
+                keep_awake(2)
+            if it == d_tr + 1:
                 turn_x(0)
-            if it == 3:
+            if it == d_tr + 2:
                 make_bias()
                 turn_x(1)
-            if it == d_q:
+            if it == d_q + 1:
                 quantize_x()
-            if 0 <= it - d_q < NT:
-                stage_q(it - d_q)
+            if 0 <= it - d_q < NT and (it - d_q) % 2 == 1:
+                stage_q(it - d_q - 1)
             for act, hg, c0, c1 in rope_at.get(it, []):
                 if act == 0:
                     rope_mul(hg, c0, c1)

from contextlib import ExitStack

import concourse.mybir as mybir
from concourse.masks import make_identity

F32 = mybir.dt.float32
BF16 = mybir.dt.bfloat16
U32 = mybir.dt.uint32
U8 = mybir.dt.uint8
I32 = mybir.dt.int32
FP8 = mybir.dt.float8_e4m3fn
FP8X4 = mybir.dt.float8_e4m3fn_x4
ACT = mybir.ActivationFunctionType
ALU = mybir.AluOpType

P = 128
SEQ = 256
HID = 2048
NH = 16
NT = 48
PASSES = 4
TWO_PI = 6.283185307179586

FLOPS = 2 * SEQ * HID * 3 * NH * P

S_HALVES = range(3, NT - 1, 2)
LAST_BACK_MATMUL = 42


def tile_selfattention_pa_kernel(tc, hidden_states, W_qkv_bytes, W_qkv_scale, b_qkv, out_0, out_1, out_2):
    nc = tc.nc
    outs = [out_0, out_1, out_2]
    with ExitStack() as ctx:
        const = ctx.enter_context(tc.tile_pool(name="const", bufs=1))
        work = ctx.enter_context(tc.tile_pool(name="work", bufs=3))
        deep = ctx.enter_context(tc.tile_pool(name="deep", bufs=3))
        castp = ctx.enter_context(tc.tile_pool(name="castp", bufs=5))
        usbp = ctx.enter_context(tc.tile_pool(name="usbp", bufs=3))
        pbp = ctx.enter_context(tc.tile_pool(name="pbp", bufs=3))
        ogp = ctx.enter_context(tc.tile_pool(name="ogp", bufs=2))
        pst = ctx.enter_context(tc.psum_pool(name="pst", bufs=5))
        psa = ctx.enter_context(tc.psum_pool(name="psa", bufs=3))
        ctx.enter_context(tc.manual_schedule())

        wrows = W_qkv_bytes.rearrange("(i p) k -> p i k", p=P)
        wv = {}

        def load_w_single(h, c):
            t = const.tile([P, HID], U8, name="wbytes_%d_%d" % (h, c))
            nc.sync.dma_start(out=t[:], in_=wrows[:, 3 * h + c, :])
            wv[(h, c)] = t[:]

        def load_w_head(h):
            t = const.tile([P, 3, HID], U8, name="wbytes_h%d" % h)
            nc.sync.dma_start(out=t[:], in_=wrows[:, 3 * h:3 * h + 3, :])
            for c in range(3):
                wv[(h, c)] = t[:, c, :]

        xraw = [const.tile([P, HID], BF16, name="xraw%d" % m) for m in range(2)]
        xsrc = hidden_states.rearrange("(m p) b k -> p m (b k)", p=P)
        braw = const.tile([P, P], BF16, name="braw")

        pos_f = const.tile([P, 2], F32, name="pos_f")
        nc.gpsimd.iota(pos_f[:], pattern=[[P, 2]], base=0, channel_multiplier=1, allow_small_or_imprecise_dtypes=True)
        zero1 = const.tile([P, 1], F32, name="zero1")
        nc.gpsimd.memset(zero1[:], 0.0)
        nc.gpsimd.memset(braw[:], 0.0)
        ident_f = const.tile([P, P], F32, name="ident_f")
        make_identity(nc, ident_f[:])
        ident_b = const.tile([P, P], BF16, name="ident_b")
        make_identity(nc, ident_b[:])

        ones = const.tile([P, P], F32, name="ones")
        nc.vector.memset(ones[:], 1.0)

        def keep_awake(n):
            for i in range(n):
                junk = psa.tile([P, P], F32, tag="acc")
                nc.tensor.matmul(junk[:], lhsT=ones[:], rhs=ones[:], start=True, stop=True)

        keep_awake(7)
        load_w_single(0, 0)
        scol = const.tile([P, 4 * PASSES], F32, name="scol")
        nc.sync.dma_start(out=scol[:].rearrange("p (g t) -> p g t", t=4), in_=W_qkv_scale.rearrange("o (g p t) -> p (o g) t", p=P, t=4))
        nc.sync.dma_start(out=braw[0:NT, :], in_=b_qkv.rearrange("(i d) -> i d", d=P))
        load_w_single(0, 1)
        for m in range(2):
            nc.sync.dma_start(out=xraw[m][:], in_=xsrc[:, m, :])
        load_w_head(1)
        load_w_single(0, 2)
        for h in range(2, NH):
            load_w_head(h)

        sct = const.tile([P, HID], F32, name="sct")
        for g in range(PASSES):
            nc.gpsimd.tensor_copy(out=sct[:, 512 * g:512 * (g + 1)].rearrange("p (r t) -> p r t", t=4),
                                  in_=scol[:, 4 * g:4 * g + 4].unsqueeze(1).to_broadcast([P, P, 4]))

        warm = const.tile([P, 1], F32, name="warm")
        nc.scalar.activation(out=warm[:], in_=zero1[:], func=ACT.Sin)
        turns = const.tile([P, 2, 16], F32, name="turns")
        for j in range(16):
            cj = (1.0 / (10000.0 ** (j / 16.0))) / TWO_PI
            nc.scalar.activation(out=turns[:, :, j:j + 1], in_=pos_f[:].unsqueeze(2), func=ACT.Copy, scale=cj)
        tflat = turns[:].rearrange("p m j -> p (m j)")
        n_i = const.tile([P, 32], I32, name="n_i")
        nc.vector.tensor_copy(out=n_i[:], in_=tflat)
        n_f = const.tile([P, 32], F32, name="n_f")
        nc.vector.tensor_copy(out=n_f[:], in_=n_i[:])
        ang = const.tile([P, 2, 32], F32, name="ang")
        nc.vector.tensor_tensor(out=ang[:, 0, :], in0=tflat, in1=n_f[:], op=ALU.subtract)
        nc.vector.tensor_scalar(out=ang[:, 1, :], in0=ang[:, 0, :], scalar1=0.25, scalar2=None, op0=ALU.add)
        aflat = ang[:].rearrange("p a j -> p (a j)")
        wr1 = const.tile([P, 64], F32, name="wr1")
        nc.vector.scalar_tensor_tensor(out=wr1[:], in0=aflat, scalar=0.5, in1=aflat, op0=ALU.is_gt, op1=ALU.subtract)
        wr2 = const.tile([P, 2, 2, 16], F32, name="wr2")
        nc.vector.scalar_tensor_tensor(out=wr2[:].rearrange("p a m j -> p (a m j)"), in0=wr1[:], scalar=0.5, in1=wr1[:],
                                       op0=ALU.is_gt, op1=ALU.subtract)
        cosT = const.tile([P, 2, 32], F32, name="cosT")
        sinT = const.tile([P, 2, 32], F32, name="sinT")

        def make_sins():
            nc.scalar.activation(out=cosT[:, :, 0:16], in_=wr2[:, 1, :, :], func=ACT.Sin, scale=TWO_PI)
            nc.scalar.activation(out=cosT[:, :, 16:32], in_=wr2[:, 1, :, :], func=ACT.Sin, scale=TWO_PI)
            nc.scalar.activation(out=sinT[:, :, 0:16], in_=wr2[:, 0, :, :], func=ACT.Sin, scale=-TWO_PI)
            nc.scalar.activation(out=sinT[:, :, 16:32], in_=wr2[:, 0, :, :], func=ACT.Sin, scale=TWO_PI)

        bias = const.tile([P, NT], F32, name="bias")

        def make_bias():
            pbias = psa.tile([P, P], BF16, tag="acc")
            nc.tensor.transpose(pbias[:], braw[:], ident_b[:])
            nc.scalar.copy(out=bias[:], in_=pbias[:, 0:NT])

        xg = const.tile([P, PASSES * SEQ * 4], BF16, name="xg", align_bytes=64)
        xgw = xg[:].bitcast(F32).rearrange("p (g s u) -> p g s u", g=PASSES, u=2)

        def turn_x(m):
            xw = xraw[m][:].bitcast(F32)
            for hf in range(2):
                pt = pst.tile([P, 2, 2, P], F32, tag="pt")
                for gg in range(2):
                    g = 2 * hf + gg
                    for u in range(2):
                        nc.tensor.transpose(pt[:, gg, u, :], xw[:, 256 * g + u:256 * (g + 1):2], ident_f[:])
                nc.scalar.copy(out=xgw[:, 2 * hf:2 * hf + 2, m * P:(m + 1) * P, :], in_=pt[:].rearrange("p g u r -> p g r u"))

        xcodes = const.tile([P, PASSES * SEQ], U32, name="xcodes", align_bytes=64)
        xscl = const.tile([P, PASSES * SEQ], U8, name="xscl", align_bytes=64)

        def quantize_x():
            for hf in range(2):
                nc.vector.quantize_mx(out=xcodes[:, 512 * hf:512 * (hf + 1)].bitcast(FP8X4),
                                      scales=xscl[:, 512 * hf:512 * (hf + 1)],
                                      in_=xg[:, 2048 * hf:2048 * (hf + 1)])

        order = []
        for hg, kind in [(0, 0), (0, 2), (1, 0), (1, 2), (2, 0), (3, 0), (2, 2), (3, 2)]:
            for hh in range(4):
                if kind == 0:
                    order.append((hg, hh, 0))
                    order.append((hg, hh, 1))
                else:
                    order.append((hg, hh, 2))
        wbf, cbs, pls, grp, codes, scl, usb, og = {}, {}, {}, {}, {}, {}, {}, {}
        ptt, accs, pbs, pairs = {}, {}, {}, {}
        ov = [o.rearrange("(m p) b h d -> p m (b h) d", p=P) for o in outs]

        def wbytes(j):
            hg, hh, c = order[j]
            return wv[(4 * hg + hh, c)]

        def stage_cast(j):
            t = castp.tile([P, HID], BF16, name="cb", align_bytes=64)
            ns = HID
            nparts = 4 if j == 0 else 1
            wd = ns // nparts
            for c0 in range(0, ns, wd):
                cs = slice(c0, c0 + wd)
                nc.scalar.copy(out=t[:, cs], in_=wbytes(j)[:, cs].bitcast(FP8))
            for c0 in range(ns, HID, 512):
                cs = slice(c0, c0 + 512)
                nc.gpsimd.tensor_copy(out=t[:, cs], in_=wbytes(j)[:, cs].bitcast(FP8))
            cbs[j] = t

        def stage_tr(j, hf):
            raw = cbs[j][:].bitcast(F32)
            pt = pst.tile([P, 2, 2, P], F32, tag="pt")
            for gg in range(2):
                g = 2 * hf + gg
                for u in range(2):
                    nc.tensor.transpose(pt[:, u, gg, :], raw[:, 256 * g + u:256 * (g + 1):2], ident_f[:])
            ptt[(j, hf)] = pt[:].rearrange("p u g r -> p (u g r)").bitcast(BF16).rearrange("p (u g r e) -> p g r u e", g=2, u=2, e=2)

        def stage_tt(j):
            if j % 2 == 0:
                pair = deep.tile([P, 2 * HID], BF16, name="grp", align_bytes=64)
                grp[j], grp[j + 1] = pair[:, 0:HID], pair[:, HID:2 * HID]
                pairs[j] = pair
            for hf in range(1 if j in S_HALVES else 2):
                nc.vector.tensor_tensor(out=grp[j][:, 1024 * hf:1024 * (hf + 1)].rearrange("p (g r u e) -> p g r u e", g=2, u=2, e=2),
                                        in0=ptt[(j, hf)],
                                        in1=sct[:, 1024 * hf:1024 * (hf + 1)].rearrange("p (g r u e) -> p g r u e", g=2, u=2, e=2),
                                        op=ALU.mult)

        def stage_s_scale(j):
            pls[j] = pbp.tile([P, 2, 4, P], BF16, name="pl")
            for gg in range(2):
                g = 2 + gg
                for t in range(4):
                    nc.scalar.activation(out=pls[j][:, gg, t, :], in_=ptt[(j, 1)][:, gg, :, t // 2, t % 2], func=ACT.Copy,
                                         scale=scol[:, 4 * g + t:4 * g + t + 1])

        def stage_weave(j):
            for gg in range(2):
                c0 = 512 * (2 + gg)
                nc.gpsimd.tensor_scalar(out=grp[j][:, c0:c0 + 512].rearrange("p (r t) -> p r t", t=4),
                                        in0=pls[j][:, gg, :, :].rearrange("p t r -> p r t"),
                                        scalar1=1.0, scalar2=0.0, op0=ALU.mult, op1=ALU.add)

        def stage_q(j):
            cd = work.tile([P, 2 * PASSES * P], U32, name="codes", align_bytes=64)
            sl = work.tile([P, 2 * PASSES * P], U8, name="scl", align_bytes=64)
            if j < NT - 2:
                nc.vector.quantize_mx(out=cd[:].bitcast(FP8X4), scales=sl[:], in_=pairs[j][:])
            else:
                for i in range(2):
                    nc.vector.quantize_mx(out=cd[:, 512 * i:512 * (i + 1)].bitcast(FP8X4), scales=sl[:, 512 * i:512 * (i + 1)],
                                          in_=grp[j + i])
            for i in range(2):
                codes[j + i] = cd[:, 512 * i:512 * (i + 1)]
                scl[j + i] = sl[:, 512 * i:512 * (i + 1)]

        def stage_mm(j):
            acc = psa.tile([P, SEQ], F32, tag="acc")
            for g in range(PASSES):
                nc.tensor.matmul_mx(out=acc[:],
                                    lhsT=codes[j][:, g * P:(g + 1) * P].bitcast(FP8X4),
                                    lhsT_scale=scl[j][:, g * P:(g + 1) * P],
                                    rhs=xcodes[:, g * SEQ:(g + 1) * SEQ].bitcast(FP8X4),
                                    rhs_scale=xscl[:, g * SEQ:(g + 1) * SEQ],
                                    start=(g == 0), stop=(g == PASSES - 1))
            accs[j] = acc

        def stage_mm_exit(j):
            hg, hh, c = order[j]
            u = usbp.tile([P, SEQ], F32, name="usb")
            i = 3 * (4 * hg + hh) + c
            nc.scalar.activation(out=u[:], in_=accs[j][:], func=ACT.Identity, bias=bias[:, i:i + 1], scale=1.0)
            usb[j] = u

        def stage_back(j):
            pb = psa.tile([P, 2, P], F32, tag="acc")
            for m in range(2):
                if j < LAST_BACK_MATMUL:
                    nc.tensor.matmul(pb[:, m, :], lhsT=usb[j][:, m * P:(m + 1) * P], rhs=ident_f[:], start=True, stop=True)
                else:
                    nc.tensor.transpose(pb[:, m, :], usb[j][:, m * P:(m + 1) * P], ident_f[:])
            pbs[j] = pb

        v_count = {}

        def stage_back_exit(j):
            hg, hh, c = order[j]
            if hg not in og:
                og[hg] = ogp.tile([P, 2, 12, P], F32, name="og")
            nc.scalar.copy(out=og[hg][:, :, 4 * c + hh, :], in_=pbs[j][:])
            if c == 2:
                if hg == 3:
                    nc.sync.dma_start(out=ov[2][:, :, 12 + hh, :], in_=og[3][:, :, 8 + hh, :])
                else:
                    v_count[hg] = v_count.get(hg, 0) + 1
                    if v_count[hg] == 4:
                        nc.sync.dma_start(out=ov[2][:, :, 4 * hg:4 * hg + 4, :], in_=og[hg][:, :, 8:12, :])

        rtmp = {}

        def rope_mul(hg, c0, c1):
            eng = nc.gpsimd
            o = og[hg]
            n = 4 * (c1 - c0)
            ts = slice(4 * c0, 4 * c1)
            ra = ogp.tile([P, 2, n, 32], F32, name="ra")
            rb = ogp.tile([P, 2, n, 32], F32, name="rb")
            eng.tensor_tensor(out=rb[:, :, :, 0:16], in0=o[:, :, ts, 16:32],
                                    in1=sinT[:, :, 0:16].unsqueeze(2).to_broadcast([P, 2, n, 16]), op=ALU.mult)
            eng.tensor_tensor(out=rb[:, :, :, 16:32], in0=o[:, :, ts, 0:16],
                                    in1=sinT[:, :, 16:32].unsqueeze(2).to_broadcast([P, 2, n, 16]), op=ALU.mult)
            eng.tensor_tensor(out=ra[:], in0=o[:, :, ts, 0:32],
                                    in1=cosT[:].unsqueeze(2).to_broadcast([P, 2, n, 32]), op=ALU.mult)
            rtmp[(hg, c0)] = (ra, rb)

        def rope_add_store(hg, c0, c1):
            eng = nc.gpsimd
            ra, rb = rtmp[(hg, c0)]
            eng.tensor_tensor(out=og[hg][:, :, 4 * c0:4 * c1, 0:32], in0=ra[:], in1=rb[:], op=ALU.add)
            for c in range(c0, c1):
                nc.sync.dma_start(out=ov[c][:, :, 4 * hg:4 * hg + 4, :], in_=og[hg][:, :, 4 * c:4 * c + 4, :])

        d_tr = 2
        d_tt = 3
        d_q = 4
        d_mm = 7
        d_e1 = 7
        d_bt = 9
        d_back = 10
        rope_at = {}
        for hg, last in ((0, 7), (1, 19), (2, 31), (3, 39)):
            rope_at[last + d_back + 1] = [(0, hg, 0, 2)]
            rope_at[last + d_back + 2] = [(1, hg, 0, 2)]
        for it in range(NT + d_back):
            if 0 <= it - d_tt < NT:
                stage_tt(it - d_tt)
            if 0 <= it - d_back < NT:
                stage_back_exit(it - d_back)
            if it - d_tt in S_HALVES:
                stage_s_scale(it - d_tt)
                stage_weave(it - d_tt)
            if it < NT:
                stage_cast(it)
            if it == 1:
                make_sins()
            if 0 <= it - d_tr < NT:
                stage_tr(it - d_tr, 0)
            if 0 <= it - d_mm < NT:
                stage_mm(it - d_mm)
            if 0 <= it - d_e1 < NT:
                stage_mm_exit(it - d_e1)
            if 0 <= it - d_bt < NT:
                stage_back(it - d_bt)
            if d_tr <= it < d_mm:
                keep_awake(2)
            if 0 <= it - d_tr < NT:
                stage_tr(it - d_tr, 1)
            if d_tr <= it < d_mm:
                keep_awake(2)
            if it == d_tr + 1:
                turn_x(0)
            if it == d_tr + 2:
                make_bias()
                turn_x(1)
            if it == d_q + 1:
                quantize_x()
            if 0 <= it - d_q < NT and (it - d_q) % 2 == 1:
                stage_q(it - d_q - 1)
            for act, hg, c0, c1 in rope_at.get(it, []):
                if act == 0:
                    rope_mul(hg, c0, c1)
                else:
                    rope_add_store(hg, c0, c1)
